import numpy as np
import ml_dtypes


def mxq(x, axis, fmt="e4m3"):
    dtype, down = {"e4m3": (ml_dtypes.float8_e4m3fn, 7), "e5m2": (ml_dtypes.float8_e5m2, 14)}[fmt]
    v = np.moveaxis(np.asarray(x, np.float32).astype(ml_dtypes.bfloat16).astype(np.float64), axis, -1)
    blocks = v.reshape(v.shape[:-1] + (-1, 32))
    amax = np.abs(blocks).max(-1, keepdims=True)
    byte = np.maximum(np.where(amax > 0, np.frexp(amax)[1] - 1 + 127, 0) - down, 1)
    scale = np.exp2(byte - 127.0)
    codes = (blocks / scale).astype(np.float32).astype(dtype).astype(np.float64)
    return np.moveaxis((codes * scale).reshape(v.shape), -1, axis)


WIDE = False


def mx_kscale(k):
    if not WIDE:
        return np.ones(k)
    levels = np.array([10, -10, 5, -5, 0])
    a = np.random.permutation(np.resize(levels, k // 512 * 4)).reshape(k // 512, 4)
    idx = np.arange(k)
    return np.exp2(a[idx // 512, idx % 128 // 32])


BF16 = ml_dtypes.bfloat16


def bf(x):
    return np.asarray(x, np.float32).astype(BF16)


def f64(x):
    return np.asarray(x).astype(np.float64)


B, N, M, A, P, W = 8, 1024, 4, 32, 4, 32


def normalize(adj):
    mx = adj + np.eye(N)[None, :, :]
    rowsum = mx.sum(axis=2)
    r_inv = 1.0 / rowsum
    r_inv = np.where(np.isinf(r_inv), 0.0, r_inv)
    return mx * r_inv[:, :, None]


def setup_inputs():
    bound = 0.5 * np.sqrt(3.0 * N / (M * A))
    s = mx_kscale(N)
    t = s / s.min()
    g = 2.0 ** np.round(np.log2(t.mean()))
    return {"x": bf(np.random.standard_normal((B, N, M, A)) * (g / t)[None, :, None, None]),
            "adj": bf(np.random.uniform(0.0, 1.0, (B, N, N)) * (4.0 / np.sqrt(N)) * t[None, None, :]),
            "weight": bf(np.random.uniform(-bound, bound, (M, P, A, W))),
            "bias": bf(np.random.uniform(0.0, 1.0, (1, 1, P, W)))}


def reference(x, adj, weight, bias):
    h = f64(x).reshape(B, N, M * A) @ f64(weight).transpose(0, 2, 1, 3).reshape(M * A, P * W)
    adj_n = normalize(f64(adj))
    agg = mxq(adj_n, 2, "e4m3") @ mxq(h, 1, "e4m3")
    return np.maximum(agg, 0.0).reshape(B, N, P, W) + f64(bias)

@@ -1,0 +1,191 @@
+from contextlib import ExitStack
+
+import concourse.bass as bass
+import concourse.mybir as mybir
+import concourse.tile as tile
+from concourse.masks import make_identity
+
+BF16 = mybir.dt.bfloat16
+F32 = mybir.dt.float32
+U32 = mybir.dt.uint32
+U8 = mybir.dt.uint8
+FP8X4 = mybir.dt.float8_e4m3fn_x4
+ALU = mybir.AluOpType
+
+B = 8
+N = 1024
+F = 128
+P = 128
+NB = N // P
+FLOPS = 2 * B * N * N * F + 2 * B * N * F * F
+
+
+def tile_spconvlayer_kernel(tc, x, adj, weight, bias, out):
+    nc = tc.nc
+    with ExitStack() as ctx:
+        const = ctx.enter_context(tc.tile_pool(name="const", bufs=1))
+        adjp = ctx.enter_context(tc.tile_pool(name="adjp", bufs=4))
+        small = ctx.enter_context(tc.tile_pool(name="small", bufs=3))
+        tmpp = ctx.enter_context(tc.tile_pool(name="tmpp", bufs=2))
+        adjnp = ctx.enter_context(tc.tile_pool(name="adjnp", bufs=6))
+        grp = ctx.enter_context(tc.tile_pool(name="grp", bufs=3))
+        codep = ctx.enter_context(tc.tile_pool(name="codep", bufs=3))
+        xtp = ctx.enter_context(tc.tile_pool(name="xtp", bufs=2))
+        outp = ctx.enter_context(tc.tile_pool(name="outp", bufs=3))
+        pst = ctx.enter_context(tc.psum_pool(name="pst", bufs=4))
+        psx = ctx.enter_context(tc.psum_pool(name="psx", bufs=2))
+        pso = ctx.enter_context(tc.psum_pool(name="pso", bufs=2))
+
+        ident = const.tile([P, P], BF16)
+        make_identity(nc, ident[:])
+        w_sb = const.tile([P, F], BF16)
+        for m in range(4):
+            nc.scalar.dma_start(
+                out=w_sb[32 * m : 32 * m + 32, :].rearrange("a (u w) -> a u w", u=4),
+                in_=weight[m].rearrange("u a w -> a u w"),
+            )
+        bias_bf = const.tile([P, F], BF16)
+        nc.scalar.dma_start(
+            out=bias_bf[:], in_=bias.rearrange("o i u w -> (o i u w)").partition_broadcast(P)
+        )
+        bias_f = const.tile([P, F], F32)
+        nc.vector.tensor_copy(out=bias_f[:], in_=bias_bf[:])
+
+        x_sb = const.tile([P, B * NB, F], BF16)
+        x_v = x.rearrange("b (j p) m a -> b p j (m a)", p=P)
+        adj_v = adj.rearrange("b (nb p) c -> b p nb c", p=P)
+        out_v = out.rearrange("b (h q p) u w -> b h p q (u w)", h=2, q=4, p=P)
+
+        h_codes = const.tile([P, B * 2 * F], U32, align_bytes=64)
+        h_scales = const.tile([P, B * 2 * F], U8, align_bytes=64)
+        junk = const.tile([P, N], BF16)
+
+        adj_tiles = {}
+
+        def load_adj(b, pieces):
+            adj_t = adjp.tile([P, N * NB + N], BF16, name="adj_t")
+            adj_tiles[b] = adj_t
+            view = adj_t[:, 0 : N * NB].rearrange("p (nb c) -> p nb c", c=N)
+            step = NB // pieces
+            for i in range(pieces):
+                nc.sync.dma_start(
+                    out=view[:, i * step : (i + 1) * step, :],
+                    in_=adj_v[b][:, i * step : (i + 1) * step, :],
+                )
+
+        def load_x(b0, b1):
+            for b in range(b0, b1):
+                nc.sync.dma_start(out=x_sb[:, b * NB : (b + 1) * NB, :], in_=x_v[b])
+
+        def h_stage(b):
+            xt_ps = psx.tile([P, NB, P], BF16, tag="xh")
+            for j in range(NB):
+                nc.tensor.transpose(xt_ps[:, j, :], x_sb[:, b * NB + j, :], ident[:])
+            x_t = xtp.tile([P, NB, P], BF16)
+            nc.scalar.copy(out=x_t[:], in_=xt_ps[:])
+            h_grouped = xtp.tile([P, 2, F, 4], BF16, align_bytes=64)
+            for g in range(2):
+                h_ps = psx.tile([P, 4, F], F32, tag="xh")
+                for t in range(4):
+                    nc.tensor.matmul(
+                        h_ps[:, t, :], lhsT=x_t[:, 4 * g + t, :], rhs=w_sb[:], start=True, stop=True
+                    )
+                nc.scalar.copy(out=h_grouped[:, g, :, :], in_=h_ps[:].rearrange("p t w -> p w t"))
+            cols = slice(b * 2 * F, (b + 1) * 2 * F)
+            nc.vector.quantize_mx(
+                out=h_codes[:, cols].bitcast(FP8X4),
+                scales=h_scales[:, cols],
+                in_=h_grouped[:].rearrange("p g w t -> p (g w t)"),
+            )
+
+        load_adj(0, 4)
+        load_x(0, 2)
+        load_adj(1, 2)
+        load_x(2, 8)
+        load_adj(2, 2)
+        load_adj(3, 2)
+
+        for b in range(B):
+            adj_t = adj_tiles[b]
+            h_stage(b)
+            rowsum = small.tile([P, NB], F32)
+            for nb in range(NB):
+                nc.vector.tensor_scalar(
+                    out=junk[:],
+                    in0=adj_t[:, nb * N : (nb + 1) * N],
+                    scalar1=1.0,
+                    scalar2=1.0,
+                    op0=ALU.mult,
+                    op1=ALU.add,
+                    accum_out=rowsum[:, nb : nb + 1],
+                )
+            r_inv = small.tile([P, NB], F32)
+            nc.vector.reciprocal(r_inv[:], rowsum[:])
+            loops = tmpp.tile([P, NB, P], F32)
+            nc.vector.tensor_tensor(
+                out=loops[:],
+                in0=adj_t[:].rearrange("p (a c) -> p a c", c=N + P)[:, :, 0:P],
+                in1=ident[:].unsqueeze(1).to_broadcast([P, NB, P]),
+                op=ALU.add,
+            )
+            for hf in range(2):
+                grouped = grp.tile([P, 4 * N], BF16, align_bytes=64)
+                for q in range(4):
+                    nb = 4 * hf + q
+                    adjn = adjnp.tile([P, N], BF16)
+                    nc.vector.tensor_scalar(
+                        out=adjn[:],
+                        in0=adj_t[:, nb * N : (nb + 1) * N],
+                        scalar1=r_inv[:, nb : nb + 1],
+                        scalar2=None,
+                        op0=ALU.mult,
+                    )
+                    nc.vector.tensor_scalar(
+                        out=adjn[:, nb * P : (nb + 1) * P],
+                        in0=loops[:, nb, :],
+                        scalar1=r_inv[:, nb : nb + 1],
+                        scalar2=None,
+                        op0=ALU.mult,
+                    )
+                    tp = pst.tile([P, 2, 4, P], BF16)
+                    for gt in range(8):
+                        nc.tensor.transpose(
+                            tp[:, gt // 4, gt % 4, :], adjn[:, gt * P : (gt + 1) * P], ident[:]
+                        )
+                    nc.scalar.copy(
+                        out=grouped[:, q * N : (q + 1) * N].rearrange(
+                            "p (g n t) -> p g n t", g=2, n=P, t=4
+                        ),
+                        in_=tp[:].rearrange("p g t n -> p g n t"),
+                    )
+                codes = codep.tile([P, N], U32, align_bytes=64)
+                scales = codep.tile([P, N], U8, align_bytes=64)
+                nc.vector.quantize_mx(
+                    out=codes[:].bitcast(FP8X4), scales=scales[:], in_=grouped[:]
+                )
+                o_ps = pso.tile([P, 4, F], F32)
+                for q in range(4):
+                    for g in range(2):
+                        a_cols = slice((2 * q + g) * P, (2 * q + g + 1) * P)
+                        h_cols = slice((2 * b + g) * F, (2 * b + g + 1) * F)
+                        nc.tensor.matmul_mx(
+                            out=o_ps[:, q, :],
+                            lhsT=codes[:, a_cols].bitcast(FP8X4),
+                            lhsT_scale=scales[:, a_cols],
+                            rhs=h_codes[:, h_cols].bitcast(FP8X4),
+                            rhs_scale=h_scales[:, h_cols],
+                            start=(g == 0),
+                            stop=(g == 1),
+                        )
+                o_sb = outp.tile([P, 4, F], F32)
+                nc.vector.scalar_tensor_tensor(
+                    out=o_sb[:],
+                    in0=o_ps[:],
+                    scalar=0.0,
+                    in1=bias_f[:].unsqueeze(1).to_broadcast([P, 4, F]),
+                    op0=ALU.max,
+                    op1=ALU.add,
+                )
+                nc.sync.dma_start(out=out_v[b, hf], in_=o_sb[:])
+            if b + 4 < B:
+                load_adj(b + 4, 2)

@@ -1,8 +1,6 @@
 from contextlib import ExitStack
 
-import concourse.bass as bass
 import concourse.mybir as mybir
-import concourse.tile as tile
 from concourse.masks import make_identity
 
 BF16 = mybir.dt.bfloat16
@@ -11,13 +9,27 @@ U32 = mybir.dt.uint32
 U8 = mybir.dt.uint8
 FP8X4 = mybir.dt.float8_e4m3fn_x4
 ALU = mybir.AluOpType
+ACT = mybir.ActivationFunctionType
 
 B = 8
 N = 1024
 F = 128
 P = 128
 NB = N // P
+ROWS = B * NB
 FLOPS = 2 * B * N * N * F + 2 * B * N * F * F
+
+MXN = 512
+GR = 512 // MXN
+HG = MXN // F
+S_ROWS = (2, 5)
+S_SLOTS = (0, 3)
+V_ROWS = tuple(nb for nb in range(NB) if nb not in S_ROWS)
+L_T = 1
+L_C = 2
+L_D = 4
+L_M = 6
+L_E = 8
 
 
 def tile_spconvlayer_kernel(tc, x, adj, weight, bias, out):
@@ -28,13 +40,13 @@ def tile_spconvlayer_kernel(tc, x, adj, weight, bias, out):
         small = ctx.enter_context(tc.tile_pool(name="small", bufs=3))
         tmpp = ctx.enter_context(tc.tile_pool(name="tmpp", bufs=2))
         adjnp = ctx.enter_context(tc.tile_pool(name="adjnp", bufs=6))
-        grp = ctx.enter_context(tc.tile_pool(name="grp", bufs=3))
-        codep = ctx.enter_context(tc.tile_pool(name="codep", bufs=3))
-        xtp = ctx.enter_context(tc.tile_pool(name="xtp", bufs=2))
+        grp = ctx.enter_context(tc.tile_pool(name="grp", bufs=6))
+        codep = ctx.enter_context(tc.tile_pool(name="codep", bufs=8))
+        xtp = ctx.enter_context(tc.tile_pool(name="xtp", bufs=4))
         outp = ctx.enter_context(tc.tile_pool(name="outp", bufs=3))
-        pst = ctx.enter_context(tc.psum_pool(name="pst", bufs=4))
-        psx = ctx.enter_context(tc.psum_pool(name="psx", bufs=2))
-        pso = ctx.enter_context(tc.psum_pool(name="pso", bufs=2))
+        pst = ctx.enter_context(tc.psum_pool(name="pst", bufs=5))
+        pso = ctx.enter_context(tc.psum_pool(name="pso", bufs=3))
+        ctx.enter_context(tc.manual_schedule())
 
         ident = const.tile([P, P], BF16)
         make_identity(nc, ident[:])
@@ -49,23 +61,34 @@ def tile_spconvlayer_kernel(tc, x, adj, weight, bias, out):
             out=bias_bf[:], in_=bias.rearrange("o i u w -> (o i u w)").partition_broadcast(P)
         )
         bias_f = const.tile([P, F], F32)
-        nc.vector.tensor_copy(out=bias_f[:], in_=bias_bf[:])
 
         x_sb = const.tile([P, B * NB, F], BF16)
         x_v = x.rearrange("b (j p) m a -> b p j (m a)", p=P)
         adj_v = adj.rearrange("b (nb p) c -> b p nb c", p=P)
         out_v = out.rearrange("b (h q p) u w -> b h p q (u w)", h=2, q=4, p=P)
 
-        h_codes = const.tile([P, B * 2 * F], U32, align_bytes=64)
-        h_scales = const.tile([P, B * 2 * F], U8, align_bytes=64)
-        junk = const.tile([P, N], BF16)
+        h_codes = const.tile([P, 2 * B * F], U32, align_bytes=64)
+        h_scales = const.tile([P, 2 * B * F], U8, align_bytes=64)
+        junk_v = const.tile([P, N], BF16)
+        junk_s = const.tile([P, N], BF16)
 
-        adj_tiles = {}
+        adj_t = {}
+        sums = {}
+        r_inv = {}
+        loops = {}
+        adjn = {}
+        tps = {}
+        grouped = {}
+        codes = {}
+        scales = {}
+        o_ps = {}
+        o_sb = {}
+        x_t = {}
+        h_grouped = {}
 
         def load_adj(b, pieces):
-            adj_t = adjp.tile([P, N * NB + N], BF16, name="adj_t")
-            adj_tiles[b] = adj_t
-            view = adj_t[:, 0 : N * NB].rearrange("p (nb c) -> p nb c", c=N)
+            adj_t[b] = adjp.tile([P, N * NB + N], BF16, name="adj_t")
+            view = adj_t[b][:, 0 : N * NB].rearrange("p (nb c) -> p nb c", c=N)
             step = NB // pieces
             for i in range(pieces):
                 nc.sync.dma_start(
@@ -73,119 +96,228 @@ def tile_spconvlayer_kernel(tc, x, adj, weight, bias, out):
                     in_=adj_v[b][:, i * step : (i + 1) * step, :],
                 )
 
-        def load_x(b0, b1):
-            for b in range(b0, b1):
-                nc.sync.dma_start(out=x_sb[:, b * NB : (b + 1) * NB, :], in_=x_v[b])
+        def load_x(b):
+            nc.sync.dma_start(out=x_sb[:, b * NB : (b + 1) * NB, :], in_=x_v[b])
 
-        def h_stage(b):
-            xt_ps = psx.tile([P, NB, P], BF16, tag="xh")
-            for j in range(NB):
-                nc.tensor.transpose(xt_ps[:, j, :], x_sb[:, b * NB + j, :], ident[:])
-            x_t = xtp.tile([P, NB, P], BF16)
-            nc.scalar.copy(out=x_t[:], in_=xt_ps[:])
-            h_grouped = xtp.tile([P, 2, F, 4], BF16, align_bytes=64)
-            for g in range(2):
-                h_ps = psx.tile([P, 4, F], F32, tag="xh")
-                for t in range(4):
-                    nc.tensor.matmul(
-                        h_ps[:, t, :], lhsT=x_t[:, 4 * g + t, :], rhs=w_sb[:], start=True, stop=True
-                    )
-                nc.scalar.copy(out=h_grouped[:, g, :, :], in_=h_ps[:].rearrange("p t w -> p w t"))
-            cols = slice(b * 2 * F, (b + 1) * 2 * F)
-            nc.vector.quantize_mx(
-                out=h_codes[:, cols].bitcast(FP8X4),
-                scales=h_scales[:, cols],
-                in_=h_grouped[:].rearrange("p g w t -> p (g w t)"),
-            )
+        def col_of(nb):
+            if nb in S_ROWS:
+                return 8 + S_ROWS.index(nb)
+            return 8 - len(V_ROWS) + V_ROWS.index(nb)
 
-        load_adj(0, 4)
-        load_x(0, 2)
-        load_adj(1, 2)
-        load_x(2, 8)
-        load_adj(2, 2)
-        load_adj(3, 2)
-
-        for b in range(B):
-            adj_t = adj_tiles[b]
-            h_stage(b)
-            rowsum = small.tile([P, NB], F32)
-            for nb in range(NB):
+        def a_row(b, nb, on_scalar):
+            if b not in sums:
+                sums[b] = small.tile([P, 16], F32, name="sums")
+            src = adj_t[b][:, nb * N : (nb + 1) * N]
+            col = col_of(nb)
+            if on_scalar:
+                nc.scalar.activation(
+                    out=junk_s[:], in_=src, func=ACT.Copy, accum_out=sums[b][:, col : col + 1]
+                )
+            else:
                 nc.vector.tensor_scalar(
-                    out=junk[:],
-                    in0=adj_t[:, nb * N : (nb + 1) * N],
+                    out=junk_v[:],
+                    in0=src,
                     scalar1=1.0,
-                    scalar2=1.0,
+                    scalar2=0.0,
                     op0=ALU.mult,
                     op1=ALU.add,
-                    accum_out=rowsum[:, nb : nb + 1],
+                    accum_out=sums[b][:, col : col + 1],
                 )
-            r_inv = small.tile([P, NB], F32)
-            nc.vector.reciprocal(r_inv[:], rowsum[:])
-            loops = tmpp.tile([P, NB, P], F32)
+
+        def self_loops(b):
+            loops[b] = tmpp.tile([P, NB, P], F32, name="loops")
             nc.vector.tensor_tensor(
-                out=loops[:],
-                in0=adj_t[:].rearrange("p (a c) -> p a c", c=N + P)[:, :, 0:P],
+                out=loops[b][:],
+                in0=adj_t[b][:].rearrange("p (a c) -> p a c", c=N + P)[:, :, 0:P],
                 in1=ident[:].unsqueeze(1).to_broadcast([P, NB, P]),
                 op=ALU.add,
             )
-            for hf in range(2):
-                grouped = grp.tile([P, 4 * N], BF16, align_bytes=64)
-                for q in range(4):
-                    nb = 4 * hf + q
-                    adjn = adjnp.tile([P, N], BF16)
-                    nc.vector.tensor_scalar(
-                        out=adjn[:],
-                        in0=adj_t[:, nb * N : (nb + 1) * N],
-                        scalar1=r_inv[:, nb : nb + 1],
-                        scalar2=None,
-                        op0=ALU.mult,
+
+        def r_calc(b):
+            lo = 8 - len(V_ROWS)
+            hi = 8 + len(S_ROWS)
+            total = small.tile([P, 16], F32, name="total")
+            nc.vector.tensor_scalar(
+                out=total[:, lo:hi], in0=sums[b][:, lo:hi], scalar1=1.0, scalar2=None, op0=ALU.add
+            )
+            r_inv[b] = small.tile([P, 16], F32, name="r_inv")
+            nc.vector.reciprocal(r_inv[b][:, lo:hi], total[:, lo:hi])
+
+        def b_row(i):
+            b = i // NB
+            nb = i % NB
+            col = col_of(nb)
+            adjn[i] = adjnp.tile([P, N], BF16, name="adjn")
+            nc.vector.tensor_scalar(
+                out=adjn[i][:],
+                in0=adj_t[b][:, nb * N : (nb + 1) * N],
+                scalar1=r_inv[b][:, col : col + 1],
+                scalar2=None,
+                op0=ALU.mult,
+            )
+            nc.vector.tensor_scalar(
+                out=adjn[i][:, nb * P : (nb + 1) * P],
+                in0=loops[b][:, nb, :],
+                scalar1=r_inv[b][:, col : col + 1],
+                scalar2=None,
+                op0=ALU.mult,
+            )
+
+        def t_row(i):
+            tps[i] = pst.tile([P, 2, 4, P], BF16, tag="tp", name="tp")
+            for gt in range(8):
+                nc.tensor.transpose(
+                    tps[i][:, gt // 4, gt % 4, :], adjn[i][:, gt * P : (gt + 1) * P], ident[:]
+                )
+
+        def c_row(i):
+            u = i // GR
+            q = i % GR
+            if q == 0:
+                grouped[u] = grp.tile([P, GR * N], BF16, align_bytes=64, name="grouped")
+            nc.scalar.copy(
+                out=grouped[u][:, q * N : (q + 1) * N].rearrange(
+                    "p (g n t) -> p g n t", g=2, n=P, t=4
+                ),
+                in_=tps[i][:].rearrange("p g t n -> p g n t"),
+            )
+
+        def d_grp(u):
+            codes[u] = codep.tile([P, GR * 2 * P], U32, align_bytes=64, name="codes")
+            scales[u] = codep.tile([P, GR * 2 * P], U8, align_bytes=64, name="scales")
+            nc.vector.quantize_mx(
+                out=codes[u][:].bitcast(FP8X4), scales=scales[u][:], in_=grouped[u][:]
+            )
+
+        def mx_grp(u):
+            b = (u * GR) // NB
+            o_ps[u] = pso.tile([P, GR, MXN], F32, name="o_ps")
+            for q in range(GR):
+                for g in range(2):
+                    a_cols = slice((2 * q + g) * P, (2 * q + g + 1) * P)
+                    h_lo = g * B * F + (b // HG) * MXN
+                    h_cols = slice(h_lo, h_lo + MXN)
+                    nc.tensor.matmul_mx(
+                        out=o_ps[u][:, q, :],
+                        lhsT=codes[u][:, a_cols].bitcast(FP8X4),
+                        lhsT_scale=scales[u][:, a_cols],
+                        rhs=h_codes[:, h_cols].bitcast(FP8X4),
+                        rhs_scale=h_scales[:, h_cols],
+                        start=(g == 0),
+                        stop=(g == 1),
                     )
-                    nc.vector.tensor_scalar(
-                        out=adjn[:, nb * P : (nb + 1) * P],
-                        in0=loops[:, nb, :],
-                        scalar1=r_inv[:, nb : nb + 1],
-                        scalar2=None,
-                        op0=ALU.mult,
+
+        def e_grp(u):
+            i0 = u * GR
+            b = i0 // NB
+            k = i0 // 4
+            q0 = i0 % 4
+            off = (b % HG) * F
+            if q0 == 0:
+                o_sb[k] = outp.tile([P, 4, F], F32, name="o_sb")
+            nc.vector.scalar_tensor_tensor(
+                out=o_sb[k][:, q0 : q0 + GR, :],
+                in0=o_ps[u][:, :, off : off + F],
+                scalar=0.0,
+                in1=bias_f[:].unsqueeze(1).to_broadcast([P, GR, F]),
+                op0=ALU.max,
+                op1=ALU.add,
+            )
+            if q0 + GR == 4:
+                nc.sync.dma_start(out=out_v[b, k % 2], in_=o_sb[k][:])
+
+        def hs1(b):
+            xt_ps = pst.tile([P, NB, P], BF16, tag="tp", name="xt_ps")
+            for j in range(NB):
+                nc.tensor.transpose(xt_ps[:, j, :], x_sb[:, b * NB + j, :], ident[:])
+            x_t[b] = xtp.tile([P, NB, P], BF16, name="x_t")
+            nc.scalar.copy(out=x_t[b][:], in_=xt_ps[:])
+
+        def hs2(b):
+            h_grouped[b] = xtp.tile([P, 2, F, 4], BF16, align_bytes=64, name="h_grouped")
+            for g in range(2):
+                h_ps = pst.tile([P, 4, F], F32, tag="tp", name="h_ps")
+                for t in range(4):
+                    nc.tensor.matmul(
+                        h_ps[:, t, :], lhsT=x_t[b][:, 4 * g + t, :], rhs=w_sb[:], start=True, stop=True
                     )
-                    tp = pst.tile([P, 2, 4, P], BF16)
-                    for gt in range(8):
-                        nc.tensor.transpose(
-                            tp[:, gt // 4, gt % 4, :], adjn[:, gt * P : (gt + 1) * P], ident[:]
-                        )
-                    nc.scalar.copy(
-                        out=grouped[:, q * N : (q + 1) * N].rearrange(
-                            "p (g n t) -> p g n t", g=2, n=P, t=4
-                        ),
-                        in_=tp[:].rearrange("p g t n -> p g n t"),
-                    )
-                codes = codep.tile([P, N], U32, align_bytes=64)
-                scales = codep.tile([P, N], U8, align_bytes=64)
+                nc.scalar.copy(
+                    out=h_grouped[b][:, g, :, :], in_=h_ps[:].rearrange("p t w -> p w t")
+                )
+
+        def hq(b):
+            for g in range(2):
+                cols = slice(g * B * F + b * F, g * B * F + (b + 1) * F)
                 nc.vector.quantize_mx(
-                    out=codes[:].bitcast(FP8X4), scales=scales[:], in_=grouped[:]
+                    out=h_codes[:, cols].bitcast(FP8X4),
+                    scales=h_scales[:, cols],
+                    in_=h_grouped[b][:, g, :, :].rearrange("p w t -> p (w t)"),
                 )
-                o_ps = pso.tile([P, 4, F], F32)
-                for q in range(4):
-                    for g in range(2):
-                        a_cols = slice((2 * q + g) * P, (2 * q + g + 1) * P)
-                        h_cols = slice((2 * b + g) * F, (2 * b + g + 1) * F)
-                        nc.tensor.matmul_mx(
-                            out=o_ps[:, q, :],
-                            lhsT=codes[:, a_cols].bitcast(FP8X4),
-                            lhsT_scale=scales[:, a_cols],
-                            rhs=h_codes[:, h_cols].bitcast(FP8X4),
-                            rhs_scale=h_scales[:, h_cols],
-                            start=(g == 0),
-                            stop=(g == 1),
-                        )
-                o_sb = outp.tile([P, 4, F], F32)
-                nc.vector.scalar_tensor_tensor(
-                    out=o_sb[:],
-                    in0=o_ps[:],
-                    scalar=0.0,
-                    in1=bias_f[:].unsqueeze(1).to_broadcast([P, 4, F]),
-                    op0=ALU.max,
-                    op1=ALU.add,
-                )
-                nc.sync.dma_start(out=out_v[b, hf], in_=o_sb[:])
-            if b + 4 < B:
-                load_adj(b + 4, 2)
+
+        h_plan = {}
+        for b in range(B):
+            if b < HG:
+                s1 = -8 + b
+                s2 = -6 + b
+                s3 = 1 + b
+            else:
+                s1 = NB * (b - HG) + 2
+                s2 = s1 + 2
+                s3 = s2 + 3
+            h_plan[(s1, 1)] = h_plan.get((s1, 1), []) + [b]
+            h_plan[(s2, 2)] = h_plan.get((s2, 2), []) + [b]
+            h_plan[(s3, 3)] = h_plan.get((s3, 3), []) + [b]
+
+        for b in range(HG):
+            load_x(b)
+        load_adj(0, 4)
+        load_adj(1, 4)
+        for b in range(HG, B):
+            load_x(b)
+        load_adj(2, 2)
+        load_adj(3, 2)
+
+        for s in range(-NB, ROWS + L_E + GR):
+            b_next = s // NB + 1
+            k = s % NB
+            if b_next == 0:
+                a_row(0, k, False)
+                if k == 7:
+                    self_loops(0)
+                    r_calc(0)
+            elif b_next < B:
+                if k in S_SLOTS:
+                    a_row(b_next, S_ROWS[S_SLOTS.index(k)], True)
+                if k < len(V_ROWS):
+                    a_row(b_next, V_ROWS[k], False)
+                if k == 6:
+                    self_loops(b_next)
+                if k == 7:
+                    r_calc(b_next)
+            if s == 1:
+                nc.vector.tensor_copy(out=bias_f[:], in_=bias_bf[:])
+            if 0 <= s < ROWS:
+                b_row(s)
+                if k == NB - 1 and s // NB + 4 < B:
+                    load_adj(s // NB + 4, 2)
+            for b in h_plan.get((s, 1), []):
+                hs1(b)
+            for b in h_plan.get((s, 2), []):
+                hs2(b)
+            i = s - L_T
+            if 0 <= i < ROWS:
+                t_row(i)
+            i = s - L_C
+            if 0 <= i < ROWS:
+                c_row(i)
+            for b in h_plan.get((s, 3), []):
+                hq(b)
+            i = s - L_D
+            if 0 <= i < ROWS and i % GR == GR - 1:
+                d_grp(i // GR)
+            i = s - L_M
+            if 0 <= i < ROWS and i % GR == GR - 1:
+                mx_grp(i // GR)
+            i = s - L_E
+            if 0 <= i < ROWS and i % GR == GR - 1:
+                e_grp(i // GR)

@@ -69,7 +69,7 @@ def tile_spconvlayer_kernel(tc, x, adj, weight, bias, out):
 
         h_codes = const.tile([P, 2 * B * F], U32, align_bytes=64)
         h_scales = const.tile([P, 2 * B * F], U8, align_bytes=64)
-        junk_v = const.tile([P, N], BF16)
+        junk_v = const.tile([P, N // 2], F32)
         junk_s = const.tile([P, N], BF16)
 
         adj_t = {}
@@ -114,11 +114,11 @@ def tile_spconvlayer_kernel(tc, x, adj, weight, bias, out):
                     out=junk_s[:], in_=src, func=ACT.Copy, accum_out=sums[b][:, col : col + 1]
                 )
             else:
-                nc.vector.tensor_scalar(
+                nc.vector.scalar_tensor_tensor(
                     out=junk_v[:],
-                    in0=src,
-                    scalar1=1.0,
-                    scalar2=0.0,
+                    in0=src[:, 0 : N // 2],
+                    scalar=1.0,
+                    in1=src[:, N // 2 : N],
                     op0=ALU.mult,
                     op1=ALU.add,
                     accum_out=sums[b][:, col : col + 1],

@@ -19,17 +19,22 @@ NB = N // P
 ROWS = B * NB
 FLOPS = 2 * B * N * N * F + 2 * B * N * F * F
 
-MXN = 512
-GR = 512 // MXN
-HG = MXN // F
-S_ROWS = (2, 5)
-S_SLOTS = (0, 3)
-V_ROWS = tuple(nb for nb in range(NB) if nb not in S_ROWS)
+S_STEADY = (7,)
+GROUP_SIZES = [4] * 15 + [2, 1, 1]
+V_COPIES = (61,)
 L_T = 1
 L_C = 2
 L_D = 4
 L_M = 6
 L_E = 8
+
+
+def s_rows_of(b):
+    if b == 0:
+        return (6, 7)
+    if b == 1:
+        return (5, 6, 7)
+    return S_STEADY
 
 
 def tile_spconvlayer_kernel(tc, x, adj, weight, bias, out):
@@ -38,14 +43,14 @@ def tile_spconvlayer_kernel(tc, x, adj, weight, bias, out):
         const = ctx.enter_context(tc.tile_pool(name="const", bufs=1))
         adjp = ctx.enter_context(tc.tile_pool(name="adjp", bufs=4))
         small = ctx.enter_context(tc.tile_pool(name="small", bufs=3))
-        tmpp = ctx.enter_context(tc.tile_pool(name="tmpp", bufs=2))
+        tmpp = ctx.enter_context(tc.tile_pool(name="tmpp", bufs=3))
         adjnp = ctx.enter_context(tc.tile_pool(name="adjnp", bufs=6))
-        grp = ctx.enter_context(tc.tile_pool(name="grp", bufs=6))
-        codep = ctx.enter_context(tc.tile_pool(name="codep", bufs=8))
-        xtp = ctx.enter_context(tc.tile_pool(name="xtp", bufs=4))
+        grp = ctx.enter_context(tc.tile_pool(name="grp", bufs=3))
+        codep = ctx.enter_context(tc.tile_pool(name="codep", bufs=3))
+        xtp = ctx.enter_context(tc.tile_pool(name="xtp", bufs=3))
         outp = ctx.enter_context(tc.tile_pool(name="outp", bufs=3))
-        pst = ctx.enter_context(tc.psum_pool(name="pst", bufs=5))
-        pso = ctx.enter_context(tc.psum_pool(name="pso", bufs=3))
+        pst = ctx.enter_context(tc.psum_pool(name="pst", bufs=6))
+        pso = ctx.enter_context(tc.psum_pool(name="pso", bufs=2))
         ctx.enter_context(tc.manual_schedule())
 
         ident = const.tile([P, P], BF16)
@@ -67,15 +72,17 @@ def tile_spconvlayer_kernel(tc, x, adj, weight, bias, out):
         adj_v = adj.rearrange("b (nb p) c -> b p nb c", p=P)
         out_v = out.rearrange("b (h q p) u w -> b h p q (u w)", h=2, q=4, p=P)
 
-        h_codes = const.tile([P, 2 * B * F], U32, align_bytes=64)
-        h_scales = const.tile([P, 2 * B * F], U8, align_bytes=64)
-        junk_v = const.tile([P, N // 2], F32)
+        h_codes = const.tile([P, B * 2 * F], U32, align_bytes=64)
+        h_scales = const.tile([P, B * 2 * F], U8, align_bytes=64)
+        junk_v = const.tile([P, N], BF16)
         junk_s = const.tile([P, N], BF16)
 
         adj_t = {}
         sums = {}
+        total = {}
         r_inv = {}
         loops = {}
+        dblk = {}
         adjn = {}
         tps = {}
         grouped = {}
@@ -86,67 +93,67 @@ def tile_spconvlayer_kernel(tc, x, adj, weight, bias, out):
         x_t = {}
         h_grouped = {}
 
-        def load_adj(b, pieces):
-            adj_t[b] = adjp.tile([P, N * NB + N], BF16, name="adj_t")
+        def load_adj(b, nb0, nb1):
+            if b not in adj_t:
+                adj_t[b] = adjp.tile([P, N * NB + N], BF16, name="adj_t")
             view = adj_t[b][:, 0 : N * NB].rearrange("p (nb c) -> p nb c", c=N)
-            step = NB // pieces
-            for i in range(pieces):
-                nc.sync.dma_start(
-                    out=view[:, i * step : (i + 1) * step, :],
-                    in_=adj_v[b][:, i * step : (i + 1) * step, :],
-                )
+            nc.sync.dma_start(out=view[:, nb0:nb1, :], in_=adj_v[b][:, nb0:nb1, :])
 
         def load_x(b):
             nc.sync.dma_start(out=x_sb[:, b * NB : (b + 1) * NB, :], in_=x_v[b])
 
-        def col_of(nb):
-            if nb in S_ROWS:
-                return 8 + S_ROWS.index(nb)
-            return 8 - len(V_ROWS) + V_ROWS.index(nb)
+        def col_of(b, nb):
+            return nb + len(s_rows_of(b))
 
-        def a_row(b, nb, on_scalar):
+        def a_row(b, nb):
             if b not in sums:
                 sums[b] = small.tile([P, 16], F32, name="sums")
+                total[b] = small.tile([P, 16], F32, name="total")
+                r_inv[b] = small.tile([P, 16], F32, name="r_inv")
+                loops[b] = tmpp.tile([P, NB, P], F32, name="loops")
+                dblk[b] = tmpp.tile([P, NB, P], BF16, name="dblk")
             src = adj_t[b][:, nb * N : (nb + 1) * N]
-            col = col_of(nb)
-            if on_scalar:
+            col = col_of(b, nb)
+            if nb in s_rows_of(b):
                 nc.scalar.activation(
                     out=junk_s[:], in_=src, func=ACT.Copy, accum_out=sums[b][:, col : col + 1]
                 )
             else:
-                nc.vector.scalar_tensor_tensor(
+                nc.vector.tensor_scalar(
                     out=junk_v[:],
-                    in0=src[:, 0 : N // 2],
-                    scalar=1.0,
-                    in1=src[:, N // 2 : N],
+                    in0=src,
+                    scalar1=1.0,
+                    scalar2=0.0,
                     op0=ALU.mult,
                     op1=ALU.add,
                     accum_out=sums[b][:, col : col + 1],
                 )
 
-        def self_loops(b):
-            loops[b] = tmpp.tile([P, NB, P], F32, name="loops")
+        def self_loops(b, nb0, nb1):
             nc.vector.tensor_tensor(
-                out=loops[b][:],
-                in0=adj_t[b][:].rearrange("p (a c) -> p a c", c=N + P)[:, :, 0:P],
-                in1=ident[:].unsqueeze(1).to_broadcast([P, NB, P]),
+                out=loops[b][:, nb0:nb1, :],
+                in0=adj_t[b][:].rearrange("p (a c) -> p a c", c=N + P)[:, nb0:nb1, 0:P],
+                in1=ident[:].unsqueeze(1).to_broadcast([P, nb1 - nb0, P]),
                 op=ALU.add,
             )
 
-        def r_calc(b):
-            lo = 8 - len(V_ROWS)
-            hi = 8 + len(S_ROWS)
-            total = small.tile([P, 16], F32, name="total")
+        def r_calc(b, lo, hi):
             nc.vector.tensor_scalar(
-                out=total[:, lo:hi], in0=sums[b][:, lo:hi], scalar1=1.0, scalar2=None, op0=ALU.add
+                out=total[b][:, lo:hi], in0=sums[b][:, lo:hi], scalar1=1.0, scalar2=None, op0=ALU.add
             )
-            r_inv[b] = small.tile([P, 16], F32, name="r_inv")
-            nc.vector.reciprocal(r_inv[b][:, lo:hi], total[:, lo:hi])
+            nc.vector.reciprocal(r_inv[b][:, lo:hi], total[b][:, lo:hi])
+            k = len(s_rows_of(b))
+            nc.vector.tensor_tensor(
+                out=dblk[b][:, lo - k : hi - k, :],
+                in0=loops[b][:, lo - k : hi - k, :],
+                in1=r_inv[b][:, lo:hi].unsqueeze(2).to_broadcast([P, hi - lo, P]),
+                op=ALU.mult,
+            )
 
         def b_row(i):
             b = i // NB
             nb = i % NB
-            col = col_of(nb)
+            col = col_of(b, nb)
             adjn[i] = adjnp.tile([P, N], BF16, name="adjn")
             nc.vector.tensor_scalar(
                 out=adjn[i][:],
@@ -155,48 +162,48 @@ def tile_spconvlayer_kernel(tc, x, adj, weight, bias, out):
                 scalar2=None,
                 op0=ALU.mult,
             )
-            nc.vector.tensor_scalar(
-                out=adjn[i][:, nb * P : (nb + 1) * P],
-                in0=loops[b][:, nb, :],
-                scalar1=r_inv[b][:, col : col + 1],
-                scalar2=None,
-                op0=ALU.mult,
-            )
 
         def t_row(i):
             tps[i] = pst.tile([P, 2, 4, P], BF16, tag="tp", name="tp")
             for gt in range(8):
-                nc.tensor.transpose(
-                    tps[i][:, gt // 4, gt % 4, :], adjn[i][:, gt * P : (gt + 1) * P], ident[:]
-                )
+                block = adjn[i][:, gt * P : (gt + 1) * P]
+                if gt == i % NB:
+                    block = dblk[i // NB][:, gt, :]
+                nc.tensor.transpose(tps[i][:, gt // 4, gt % 4, :], block, ident[:])
+
+        group_of = {}
+        first_row = []
+        for u in range(len(GROUP_SIZES)):
+            first_row.append(sum(GROUP_SIZES[:u]))
+            for q in range(GROUP_SIZES[u]):
+                group_of[first_row[u] + q] = u
 
         def c_row(i):
-            u = i // GR
-            q = i % GR
+            u = group_of[i]
+            q = i - first_row[u]
             if q == 0:
-                grouped[u] = grp.tile([P, GR * N], BF16, align_bytes=64, name="grouped")
-            nc.scalar.copy(
-                out=grouped[u][:, q * N : (q + 1) * N].rearrange(
-                    "p (g n t) -> p g n t", g=2, n=P, t=4
-                ),
-                in_=tps[i][:].rearrange("p g t n -> p g n t"),
-            )
+                grouped[u] = grp.tile([P, GROUP_SIZES[u] * N], BF16, align_bytes=64, name="grouped")
+            dst = grouped[u][:, q * N : (q + 1) * N].rearrange("p (g n t) -> p g n t", g=2, n=P, t=4)
+            src = tps[i][:].rearrange("p g t n -> p g n t")
+            if i in V_COPIES:
+                nc.vector.tensor_copy(out=dst, in_=src)
+            else:
+                nc.scalar.copy(out=dst, in_=src)
 
         def d_grp(u):
-            codes[u] = codep.tile([P, GR * 2 * P], U32, align_bytes=64, name="codes")
-            scales[u] = codep.tile([P, GR * 2 * P], U8, align_bytes=64, name="scales")
+            codes[u] = codep.tile([P, GROUP_SIZES[u] * 2 * P], U32, align_bytes=64, name="codes")
+            scales[u] = codep.tile([P, GROUP_SIZES[u] * 2 * P], U8, align_bytes=64, name="scales")
             nc.vector.quantize_mx(
                 out=codes[u][:].bitcast(FP8X4), scales=scales[u][:], in_=grouped[u][:]
             )
 
         def mx_grp(u):
-            b = (u * GR) // NB
-            o_ps[u] = pso.tile([P, GR, MXN], F32, name="o_ps")
-            for q in range(GR):
+            b = first_row[u] // NB
+            o_ps[u] = pso.tile([P, GROUP_SIZES[u], F], F32, name="o_ps")
+            for q in range(GROUP_SIZES[u]):
                 for g in range(2):
                     a_cols = slice((2 * q + g) * P, (2 * q + g + 1) * P)
-                    h_lo = g * B * F + (b // HG) * MXN
-                    h_cols = slice(h_lo, h_lo + MXN)
+                    h_cols = slice((2 * b + g) * F, (2 * b + g + 1) * F)
                     nc.tensor.matmul_mx(
                         out=o_ps[u][:, q, :],
                         lhsT=codes[u][:, a_cols].bitcast(FP8X4),
@@ -208,23 +215,20 @@ def tile_spconvlayer_kernel(tc, x, adj, weight, bias, out):
                     )
 
         def e_grp(u):
-            i0 = u * GR
+            i0 = first_row[u]
+            size = GROUP_SIZES[u]
             b = i0 // NB
-            k = i0 // 4
             q0 = i0 % 4
-            off = (b % HG) * F
-            if q0 == 0:
-                o_sb[k] = outp.tile([P, 4, F], F32, name="o_sb")
+            o_sb[u] = outp.tile([P, size, F], F32, name="o_sb")
             nc.vector.scalar_tensor_tensor(
-                out=o_sb[k][:, q0 : q0 + GR, :],
-                in0=o_ps[u][:, :, off : off + F],
+                out=o_sb[u][:],
+                in0=o_ps[u][:],
                 scalar=0.0,
-                in1=bias_f[:].unsqueeze(1).to_broadcast([P, GR, F]),
+                in1=bias_f[:].unsqueeze(1).to_broadcast([P, size, F]),
                 op0=ALU.max,
                 op1=ALU.add,
             )
-            if q0 + GR == 4:
-                nc.sync.dma_start(out=out_v[b, k % 2], in_=o_sb[k][:])
+            nc.sync.dma_start(out=out_v[b, (i0 // 4) % 2][:, q0 : q0 + size, :], in_=o_sb[u][:])
 
         def hs1(b):
             xt_ps = pst.tile([P, NB, P], BF16, tag="tp", name="xt_ps")
@@ -246,78 +250,103 @@ def tile_spconvlayer_kernel(tc, x, adj, weight, bias, out):
                 )
 
         def hq(b):
-            for g in range(2):
-                cols = slice(g * B * F + b * F, g * B * F + (b + 1) * F)
-                nc.vector.quantize_mx(
-                    out=h_codes[:, cols].bitcast(FP8X4),
-                    scales=h_scales[:, cols],
-                    in_=h_grouped[b][:, g, :, :].rearrange("p w t -> p (w t)"),
-                )
+            cols = slice(2 * b * F, 2 * (b + 1) * F)
+            nc.vector.quantize_mx(
+                out=h_codes[:, cols].bitcast(FP8X4),
+                scales=h_scales[:, cols],
+                in_=h_grouped[b][:].rearrange("p g w t -> p (g w t)"),
+            )
 
-        h_plan = {}
-        for b in range(B):
-            if b < HG:
-                s1 = -8 + b
-                s2 = -6 + b
-                s3 = 1 + b
+        plan = {}
+
+        def put(step, kind, args):
+            plan[(step, kind)] = plan.get((step, kind), []) + [args]
+
+        for unit in ((0, 1), (1, 2), (2, 4), (4, 8)):
+            cols = [col_of(0, nb) for nb in range(unit[0], unit[1])]
+            for nb in range(unit[0], unit[1]):
+                if nb in s_rows_of(0):
+                    put(2, "as", (0, nb))
+                else:
+                    put(unit[0], "a", (0, nb))
+            put(unit[0], "loops", (0, unit[0], unit[1]))
+            put(unit[0], "r", (0, min(cols), max(cols) + 1))
+        for b in range(1, B):
+            s_rows = s_rows_of(b)
+            v_rows = [r for r in range(NB) if r not in s_rows]
+            base = NB * (b - 1)
+            if b == 1:
+                s_slots = (5, 6, 6)
+                v_slots = (4, 5, 5, 6, 7)
             else:
-                s1 = NB * (b - HG) + 2
-                s2 = s1 + 2
-                s3 = s2 + 3
-            h_plan[(s1, 1)] = h_plan.get((s1, 1), []) + [b]
-            h_plan[(s2, 2)] = h_plan.get((s2, 2), []) + [b]
-            h_plan[(s3, 3)] = h_plan.get((s3, 3), []) + [b]
+                s_slots = (2, 4)
+                v_slots = (0, 1, 2, 3, 4, 5, 6)
+            for idx in range(len(s_rows)):
+                put(base + s_slots[idx], "as", (b, s_rows[idx]))
+            for idx in range(len(v_rows)):
+                put(base + v_slots[idx], "a", (b, v_rows[idx]))
+            put(base + 6, "loops", (b, 0, NB))
+            put(base + 7, "r", (b, len(s_rows), len(s_rows) + NB))
+        for b in range(B):
+            put(2 * b + 2, "hs1", b)
+            put(2 * b + 3, "hs2", b)
+            put(2 * b + 6, "hq", b)
 
-        for b in range(HG):
+        load_adj(0, 0, 1)
+        load_adj(0, 1, 2)
+        load_x(0)
+        load_adj(0, 2, 3)
+        load_adj(0, 3, 4)
+        load_x(1)
+        load_adj(0, 4, 6)
+        load_adj(0, 6, 8)
+        load_adj(1, 0, 2)
+        load_adj(1, 2, 4)
+        load_x(2)
+        load_adj(1, 4, 6)
+        load_adj(1, 6, 8)
+        load_x(3)
+        for b in range(4, B):
             load_x(b)
-        load_adj(0, 4)
-        load_adj(1, 4)
-        for b in range(HG, B):
-            load_x(b)
-        load_adj(2, 2)
-        load_adj(3, 2)
+        load_adj(2, 0, 4)
+        load_adj(2, 4, 8)
+        load_adj(3, 0, 4)
+        load_adj(3, 4, 8)
 
-        for s in range(-NB, ROWS + L_E + GR):
-            b_next = s // NB + 1
-            k = s % NB
-            if b_next == 0:
-                a_row(0, k, False)
-                if k == 7:
-                    self_loops(0)
-                    r_calc(0)
-            elif b_next < B:
-                if k in S_SLOTS:
-                    a_row(b_next, S_ROWS[S_SLOTS.index(k)], True)
-                if k < len(V_ROWS):
-                    a_row(b_next, V_ROWS[k], False)
-                if k == 6:
-                    self_loops(b_next)
-                if k == 7:
-                    r_calc(b_next)
-            if s == 1:
+        for s in range(0, ROWS + L_E + 1):
+            for args in plan.get((s, "a"), []):
+                a_row(args[0], args[1])
+            for args in plan.get((s, "loops"), []):
+                self_loops(args[0], args[1], args[2])
+            for args in plan.get((s, "r"), []):
+                r_calc(args[0], args[1], args[2])
+            if s == 2:
                 nc.vector.tensor_copy(out=bias_f[:], in_=bias_bf[:])
-            if 0 <= s < ROWS:
+            if s < ROWS:
                 b_row(s)
-                if k == NB - 1 and s // NB + 4 < B:
-                    load_adj(s // NB + 4, 2)
-            for b in h_plan.get((s, 1), []):
-                hs1(b)
-            for b in h_plan.get((s, 2), []):
-                hs2(b)
+                if s % NB == NB - 1 and s // NB + 4 < B:
+                    load_adj(s // NB + 4, 0, 4)
+                    load_adj(s // NB + 4, 4, 8)
             i = s - L_T
             if 0 <= i < ROWS:
                 t_row(i)
             i = s - L_C
             if 0 <= i < ROWS:
                 c_row(i)
-            for b in h_plan.get((s, 3), []):
+            for args in plan.get((s, "as"), []):
+                a_row(args[0], args[1])
+            for b in plan.get((s, "hs1"), []):
+                hs1(b)
+            for b in plan.get((s, "hs2"), []):
+                hs2(b)
+            for b in plan.get((s, "hq"), []):
                 hq(b)
             i = s - L_D
-            if 0 <= i < ROWS and i % GR == GR - 1:
-                d_grp(i // GR)
+            if 0 <= i < ROWS and group_of.get(i + 1, -1) != group_of[i]:
+                d_grp(group_of[i])
             i = s - L_M
-            if 0 <= i < ROWS and i % GR == GR - 1:
-                mx_grp(i // GR)
+            if 0 <= i < ROWS and group_of.get(i + 1, -1) != group_of[i]:
+                mx_grp(group_of[i])
             i = s - L_E
-            if 0 <= i < ROWS and i % GR == GR - 1:
-                e_grp(i // GR)
+            if 0 <= i < ROWS and group_of.get(i + 1, -1) != group_of[i]:
+                e_grp(group_of[i])

@@ -25,8 +25,10 @@ V_COPIES = (61,)
 L_T = 1
 L_C = 2
 L_D = 4
-L_M = 6
-L_E = 8
+L_M = 8
+L_E = 10
+FILL_ROWS = 52
+FILL = (512, 256)
 
 
 def s_rows_of(b):
@@ -34,6 +36,8 @@ def s_rows_of(b):
         return (6, 7)
     if b == 1:
         return (5, 6, 7)
+    if b % 2 == 1:
+        return (6, 7)
     return S_STEADY
 
 
@@ -49,8 +53,8 @@ def tile_spconvlayer_kernel(tc, x, adj, weight, bias, out):
         codep = ctx.enter_context(tc.tile_pool(name="codep", bufs=3))
         xtp = ctx.enter_context(tc.tile_pool(name="xtp", bufs=3))
         outp = ctx.enter_context(tc.tile_pool(name="outp", bufs=3))
-        pst = ctx.enter_context(tc.psum_pool(name="pst", bufs=6))
-        pso = ctx.enter_context(tc.psum_pool(name="pso", bufs=2))
+        pst = ctx.enter_context(tc.psum_pool(name="pst", bufs=5))
+        pso = ctx.enter_context(tc.psum_pool(name="pso", bufs=3))
         ctx.enter_context(tc.manual_schedule())
 
         ident = const.tile([P, P], BF16)
@@ -197,21 +201,40 @@ def tile_spconvlayer_kernel(tc, x, adj, weight, bias, out):
                 out=codes[u][:].bitcast(FP8X4), scales=scales[u][:], in_=grouped[u][:]
             )
 
-        def mx_grp(u):
-            b = first_row[u] // NB
-            o_ps[u] = pso.tile([P, GROUP_SIZES[u], F], F32, name="o_ps")
-            for q in range(GROUP_SIZES[u]):
-                for g in range(2):
-                    a_cols = slice((2 * q + g) * P, (2 * q + g + 1) * P)
-                    h_cols = slice((2 * b + g) * F, (2 * b + g + 1) * F)
+        def bank_of(u):
+            if u not in o_ps:
+                o_ps[u] = pso.tile([P, 4, F], F32, name="o_ps")
+            return o_ps[u]
+
+        def mx_row(i):
+            u = group_of[i]
+            q = i - first_row[u]
+            b = i // NB
+            bank = bank_of(u)
+            for g in range(2):
+                a_cols = slice((2 * q + g) * P, (2 * q + g + 1) * P)
+                h_cols = slice((2 * b + g) * F, (2 * b + g + 1) * F)
+                nc.tensor.matmul_mx(
+                    out=bank[:, q, :],
+                    lhsT=codes[u][:, a_cols].bitcast(FP8X4),
+                    lhsT_scale=scales[u][:, a_cols],
+                    rhs=h_codes[:, h_cols].bitcast(FP8X4),
+                    rhs_scale=h_scales[:, h_cols],
+                    start=(g == 0),
+                    stop=(g == 1),
+                )
+            if i < FILL_ROWS:
+                spare = bank_of(u + 1)[:].rearrange("p q f -> p (q f)")
+                a_cols = slice(2 * q * P, (2 * q + 1) * P)
+                for width in FILL:
                     nc.tensor.matmul_mx(
-                        out=o_ps[u][:, q, :],
+                        out=spare[:, 0:width],
                         lhsT=codes[u][:, a_cols].bitcast(FP8X4),
                         lhsT_scale=scales[u][:, a_cols],
-                        rhs=h_codes[:, h_cols].bitcast(FP8X4),
-                        rhs_scale=h_scales[:, h_cols],
-                        start=(g == 0),
-                        stop=(g == 1),
+                        rhs=h_codes[:, 0:width].bitcast(FP8X4),
+                        rhs_scale=h_scales[:, 0:width],
+                        start=True,
+                        stop=True,
                     )
 
         def e_grp(u):
@@ -222,7 +245,7 @@ def tile_spconvlayer_kernel(tc, x, adj, weight, bias, out):
             o_sb[u] = outp.tile([P, size, F], F32, name="o_sb")
             nc.vector.scalar_tensor_tensor(
                 out=o_sb[u][:],
-                in0=o_ps[u][:],
+                in0=o_ps[u][:, 0:size, :],
                 scalar=0.0,
                 in1=bias_f[:].unsqueeze(1).to_broadcast([P, size, F]),
                 op0=ALU.max,
@@ -345,8 +368,8 @@ def tile_spconvlayer_kernel(tc, x, adj, weight, bias, out):
             if 0 <= i < ROWS and group_of.get(i + 1, -1) != group_of[i]:
                 d_grp(group_of[i])
             i = s - L_M
-            if 0 <= i < ROWS and group_of.get(i + 1, -1) != group_of[i]:
-                mx_grp(group_of[i])
+            if 0 <= i < ROWS:
+                mx_row(i)
             i = s - L_E
             if 0 <= i < ROWS and group_of.get(i + 1, -1) != group_of[i]:
                 e_grp(group_of[i])

@@ -19,7 +19,7 @@ NB = N // P
 ROWS = B * NB
 FLOPS = 2 * B * N * N * F + 2 * B * N * F * F
 
-S_STEADY = (7,)
+S_STEADY = ()
 GROUP_SIZES = [4] * 15 + [2, 1, 1]
 V_COPIES = (61,)
 L_T = 1
@@ -36,8 +36,6 @@ def s_rows_of(b):
         return (6, 7)
     if b == 1:
         return (5, 6, 7)
-    if b % 2 == 1:
-        return (6, 7)
     return S_STEADY
 
 
@@ -303,7 +301,7 @@ def tile_spconvlayer_kernel(tc, x, adj, weight, bias, out):
                 v_slots = (4, 5, 5, 6, 7)
             else:
                 s_slots = (2, 4)
-                v_slots = (0, 1, 2, 3, 4, 5, 6)
+                v_slots = (0, 1, 2, 3, 4, 5, 6, 7)
             for idx in range(len(s_rows)):
                 put(base + s_slots[idx], "as", (b, s_rows[idx]))
             for idx in range(len(v_rows)):

@@ -17,301 +17,225 @@ F = 128
 P = 128
 NB = N // P
 ROWS = B * NB
+PASSES = N // (4 * P)
 FLOPS = 2 * B * N * N * F + 2 * B * N * F * F
 
-S_STEADY = ()
-GROUP_SIZES = [4] * 15 + [2, 1, 1]
-V_COPIES = (61,)
-L_T = 1
-L_C = 2
-L_D = 4
-L_M = 8
-L_E = 10
-FILL_ROWS = 52
-FILL = (512, 256)
-
-
-def s_rows_of(b):
-    if b == 0:
-        return (6, 7)
-    if b == 1:
-        return (5, 6, 7)
-    return S_STEADY
+VECTOR_SUMS = 6
+GROUP_SIZES = [4] * (ROWS // 4 - 1) + [2, 1, 1]
+LAG_TRANSPOSE = 1
+LAG_COPY = 2
+LAG_QUANTISE = 4
+LAG_MATMUL = 6
+LAG_OUTPUT = 8
 
 
 def tile_spconvlayer_kernel(tc, x, adj, weight, bias, out):
     nc = tc.nc
     with ExitStack() as ctx:
         const = ctx.enter_context(tc.tile_pool(name="const", bufs=1))
-        adjp = ctx.enter_context(tc.tile_pool(name="adjp", bufs=4))
-        small = ctx.enter_context(tc.tile_pool(name="small", bufs=3))
-        tmpp = ctx.enter_context(tc.tile_pool(name="tmpp", bufs=3))
-        adjnp = ctx.enter_context(tc.tile_pool(name="adjnp", bufs=6))
-        grp = ctx.enter_context(tc.tile_pool(name="grp", bufs=3))
-        codep = ctx.enter_context(tc.tile_pool(name="codep", bufs=3))
-        xtp = ctx.enter_context(tc.tile_pool(name="xtp", bufs=3))
-        outp = ctx.enter_context(tc.tile_pool(name="outp", bufs=3))
-        pst = ctx.enter_context(tc.psum_pool(name="pst", bufs=5))
-        pso = ctx.enter_context(tc.psum_pool(name="pso", bufs=3))
+        adj_pool = ctx.enter_context(tc.tile_pool(name="adj_pool", bufs=4))
+        norm_pool = ctx.enter_context(tc.tile_pool(name="norm_pool", bufs=3))
+        scaled_pool = ctx.enter_context(tc.tile_pool(name="scaled_pool", bufs=6))
+        group_pool = ctx.enter_context(tc.tile_pool(name="group_pool", bufs=3))
+        h_pool = ctx.enter_context(tc.tile_pool(name="h_pool", bufs=3))
+        turn_psum = ctx.enter_context(tc.psum_pool(name="turn_psum", bufs=6))
+        product_psum = ctx.enter_context(tc.psum_pool(name="product_psum", bufs=2))
         ctx.enter_context(tc.manual_schedule())
 
-        ident = const.tile([P, P], BF16)
-        make_identity(nc, ident[:])
+        x_view = x.rearrange("b (j p) m a -> b p j (m a)", p=P)
+        adj_view = adj.rearrange("b (nb p) c -> b p nb c", p=P)
+        out_view = out.rearrange("b (nb p) u w -> b p nb (u w)", p=P)
+
+        identity = const.tile([P, P], BF16)
+        make_identity(nc, identity[:])
         w_sb = const.tile([P, F], BF16)
         for m in range(4):
             nc.scalar.dma_start(
                 out=w_sb[32 * m : 32 * m + 32, :].rearrange("a (u w) -> a u w", u=4),
                 in_=weight[m].rearrange("u a w -> a u w"),
             )
-        bias_bf = const.tile([P, F], BF16)
+        bias_bf16 = const.tile([P, F], BF16)
         nc.scalar.dma_start(
-            out=bias_bf[:], in_=bias.rearrange("o i u w -> (o i u w)").partition_broadcast(P)
+            out=bias_bf16[:], in_=bias.rearrange("o i u w -> (o i u w)").partition_broadcast(P)
         )
-        bias_f = const.tile([P, F], F32)
+        bias_f32 = const.tile([P, F], F32)
+        x_sb = const.tile([P, B, NB, F], BF16)
+        h_codes = const.tile([P, B * PASSES * F], U32, align_bytes=64)
+        h_scales = const.tile([P, B * PASSES * F], U8, align_bytes=64)
+        unused_vector = const.tile([P, N], BF16)
+        unused_scalar = const.tile([P, N], BF16)
 
-        x_sb = const.tile([P, B * NB, F], BF16)
-        x_v = x.rearrange("b (j p) m a -> b p j (m a)", p=P)
-        adj_v = adj.rearrange("b (nb p) c -> b p nb c", p=P)
-        out_v = out.rearrange("b (h q p) u w -> b h p q (u w)", h=2, q=4, p=P)
-
-        h_codes = const.tile([P, B * 2 * F], U32, align_bytes=64)
-        h_scales = const.tile([P, B * 2 * F], U8, align_bytes=64)
-        junk_v = const.tile([P, N], BF16)
-        junk_s = const.tile([P, N], BF16)
-
-        adj_t = {}
+        adj_sb = {}
         sums = {}
-        total = {}
-        r_inv = {}
-        loops = {}
-        dblk = {}
-        adjn = {}
-        tps = {}
+        r = {}
+        with_loops = {}
+        diagonal = {}
+        x_turned = {}
+        h_grouped = {}
+        scaled = {}
+        turned = {}
         grouped = {}
         codes = {}
         scales = {}
-        o_ps = {}
-        o_sb = {}
-        x_t = {}
-        h_grouped = {}
+        product = {}
 
-        def load_adj(b, nb0, nb1):
-            if b not in adj_t:
-                adj_t[b] = adjp.tile([P, N * NB + N], BF16, name="adj_t")
-            view = adj_t[b][:, 0 : N * NB].rearrange("p (nb c) -> p nb c", c=N)
-            nc.sync.dma_start(out=view[:, nb0:nb1, :], in_=adj_v[b][:, nb0:nb1, :])
+        first_row = [sum(GROUP_SIZES[:u]) for u in range(len(GROUP_SIZES))]
+        group_of = {}
+        for u in range(len(GROUP_SIZES)):
+            for q in range(GROUP_SIZES[u]):
+                group_of[first_row[u] + q] = u
+
+        def ends_group(i):
+            return 0 <= i < ROWS and group_of.get(i + 1, -1) != group_of[i]
+
+        def load_adj(b, lo, hi):
+            if b not in adj_sb:
+                adj_sb[b] = adj_pool.tile([P, (NB + 1) * N], BF16, name="adj_sb")
+            rows = adj_sb[b][:, 0 : NB * N].rearrange("p (nb c) -> p nb c", c=N)
+            nc.sync.dma_start(out=rows[:, lo:hi, :], in_=adj_view[b][:, lo:hi, :])
 
         def load_x(b):
-            nc.sync.dma_start(out=x_sb[:, b * NB : (b + 1) * NB, :], in_=x_v[b])
+            nc.sync.dma_start(out=x_sb[:, b, :, :], in_=x_view[b])
 
-        def col_of(b, nb):
-            return nb + len(s_rows_of(b))
+        def column(nb):
+            return nb + 8 - VECTOR_SUMS
 
-        def a_row(b, nb):
+        def sum_rows(b, nb):
             if b not in sums:
-                sums[b] = small.tile([P, 16], F32, name="sums")
-                total[b] = small.tile([P, 16], F32, name="total")
-                r_inv[b] = small.tile([P, 16], F32, name="r_inv")
-                loops[b] = tmpp.tile([P, NB, P], F32, name="loops")
-                dblk[b] = tmpp.tile([P, NB, P], BF16, name="dblk")
-            src = adj_t[b][:, nb * N : (nb + 1) * N]
-            col = col_of(b, nb)
-            if nb in s_rows_of(b):
-                nc.scalar.activation(
-                    out=junk_s[:], in_=src, func=ACT.Copy, accum_out=sums[b][:, col : col + 1]
-                )
-            else:
+                sums[b] = norm_pool.tile([P, 16], F32, name="sums")
+            rows = adj_sb[b][:, nb * N : (nb + 1) * N]
+            total = sums[b][:, column(nb) : column(nb) + 1]
+            if nb < VECTOR_SUMS:
                 nc.vector.tensor_scalar(
-                    out=junk_v[:],
-                    in0=src,
+                    out=unused_vector[:],
+                    in0=rows,
                     scalar1=1.0,
-                    scalar2=0.0,
+                    scalar2=1.0,
                     op0=ALU.mult,
                     op1=ALU.add,
-                    accum_out=sums[b][:, col : col + 1],
+                    accum_out=total,
+                )
+            else:
+                nc.scalar.activation(
+                    out=unused_scalar[:], in_=rows, func=ACT.Copy, bias=1.0 / N, accum_out=total
                 )
 
-        def self_loops(b, nb0, nb1):
+        def add_self_loops(b, lo, hi):
+            if b not in with_loops:
+                with_loops[b] = norm_pool.tile([P, NB, P], F32, name="with_loops")
             nc.vector.tensor_tensor(
-                out=loops[b][:, nb0:nb1, :],
-                in0=adj_t[b][:].rearrange("p (a c) -> p a c", c=N + P)[:, nb0:nb1, 0:P],
-                in1=ident[:].unsqueeze(1).to_broadcast([P, nb1 - nb0, P]),
+                out=with_loops[b][:, lo:hi, :],
+                in0=adj_sb[b][:].rearrange("p (nb c) -> p nb c", c=N + P)[:, lo:hi, 0:P],
+                in1=identity[:].unsqueeze(1).to_broadcast([P, hi - lo, P]),
                 op=ALU.add,
             )
 
-        def r_calc(b, lo, hi):
-            nc.vector.tensor_scalar(
-                out=total[b][:, lo:hi], in0=sums[b][:, lo:hi], scalar1=1.0, scalar2=None, op0=ALU.add
-            )
-            nc.vector.reciprocal(r_inv[b][:, lo:hi], total[b][:, lo:hi])
-            k = len(s_rows_of(b))
+        def invert_sums(b, lo, hi):
+            if b not in r:
+                r[b] = norm_pool.tile([P, 16], F32, name="r")
+            nc.vector.reciprocal(r[b][:, column(lo) : column(hi)], sums[b][:, column(lo) : column(hi)])
+
+        def scale_diagonal(b, lo, hi):
+            if b not in diagonal:
+                diagonal[b] = norm_pool.tile([P, NB, P], BF16, name="diagonal")
             nc.vector.tensor_tensor(
-                out=dblk[b][:, lo - k : hi - k, :],
-                in0=loops[b][:, lo - k : hi - k, :],
-                in1=r_inv[b][:, lo:hi].unsqueeze(2).to_broadcast([P, hi - lo, P]),
+                out=diagonal[b][:, lo:hi, :],
+                in0=with_loops[b][:, lo:hi, :],
+                in1=r[b][:, column(lo) : column(hi)].unsqueeze(2).to_broadcast([P, hi - lo, P]),
                 op=ALU.mult,
             )
 
-        def b_row(i):
-            b = i // NB
-            nb = i % NB
-            col = col_of(b, nb)
-            adjn[i] = adjnp.tile([P, N], BF16, name="adjn")
+        def scale_rows(i):
+            b, nb = divmod(i, NB)
+            scaled[i] = scaled_pool.tile([P, N], BF16, name="scaled")
             nc.vector.tensor_scalar(
-                out=adjn[i][:],
-                in0=adj_t[b][:, nb * N : (nb + 1) * N],
-                scalar1=r_inv[b][:, col : col + 1],
+                out=scaled[i][:],
+                in0=adj_sb[b][:, nb * N : (nb + 1) * N],
+                scalar1=r[b][:, column(nb) : column(nb) + 1],
                 scalar2=None,
                 op0=ALU.mult,
             )
 
-        def t_row(i):
-            tps[i] = pst.tile([P, 2, 4, P], BF16, tag="tp", name="tp")
-            for gt in range(8):
-                block = adjn[i][:, gt * P : (gt + 1) * P]
-                if gt == i % NB:
-                    block = dblk[i // NB][:, gt, :]
-                nc.tensor.transpose(tps[i][:, gt // 4, gt % 4, :], block, ident[:])
+        def transpose_rows(i):
+            b, nb = divmod(i, NB)
+            turned[i] = turn_psum.tile([P, PASSES, 4, P], BF16, tag="turn", name="turned")
+            for block in range(NB):
+                source = scaled[i][:, block * P : (block + 1) * P]
+                if block == nb:
+                    source = diagonal[b][:, nb, :]
+                nc.tensor.transpose(turned[i][:, block // 4, block % 4, :], source, identity[:])
 
-        group_of = {}
-        first_row = []
-        for u in range(len(GROUP_SIZES)):
-            first_row.append(sum(GROUP_SIZES[:u]))
-            for q in range(GROUP_SIZES[u]):
-                group_of[first_row[u] + q] = u
-
-        def c_row(i):
+        def copy_rows(i):
             u = group_of[i]
             q = i - first_row[u]
             if q == 0:
-                grouped[u] = grp.tile([P, GROUP_SIZES[u] * N], BF16, align_bytes=64, name="grouped")
-            dst = grouped[u][:, q * N : (q + 1) * N].rearrange("p (g n t) -> p g n t", g=2, n=P, t=4)
-            src = tps[i][:].rearrange("p g t n -> p g n t")
-            if i in V_COPIES:
-                nc.vector.tensor_copy(out=dst, in_=src)
-            else:
-                nc.scalar.copy(out=dst, in_=src)
-
-        def d_grp(u):
-            codes[u] = codep.tile([P, GROUP_SIZES[u] * 2 * P], U32, align_bytes=64, name="codes")
-            scales[u] = codep.tile([P, GROUP_SIZES[u] * 2 * P], U8, align_bytes=64, name="scales")
-            nc.vector.quantize_mx(
-                out=codes[u][:].bitcast(FP8X4), scales=scales[u][:], in_=grouped[u][:]
+                grouped[u] = group_pool.tile([P, GROUP_SIZES[u] * N], BF16, align_bytes=64, name="grouped")
+            nc.scalar.copy(
+                out=grouped[u][:, q * N : (q + 1) * N].rearrange("p (g n t) -> p g n t", g=PASSES, t=4),
+                in_=turned[i][:].rearrange("p g t n -> p g n t"),
             )
 
-        def bank_of(u):
-            if u not in o_ps:
-                o_ps[u] = pso.tile([P, 4, F], F32, name="o_ps")
-            return o_ps[u]
+        def quantise_group(u):
+            width = GROUP_SIZES[u] * PASSES * P
+            codes[u] = group_pool.tile([P, width], U32, align_bytes=64, name="codes")
+            scales[u] = group_pool.tile([P, width], U8, align_bytes=64, name="scales")
+            nc.vector.quantize_mx(out=codes[u][:].bitcast(FP8X4), scales=scales[u][:], in_=grouped[u][:])
 
-        def mx_row(i):
-            u = group_of[i]
-            q = i - first_row[u]
-            b = i // NB
-            bank = bank_of(u)
-            for g in range(2):
-                a_cols = slice((2 * q + g) * P, (2 * q + g + 1) * P)
-                h_cols = slice((2 * b + g) * F, (2 * b + g + 1) * F)
-                nc.tensor.matmul_mx(
-                    out=bank[:, q, :],
-                    lhsT=codes[u][:, a_cols].bitcast(FP8X4),
-                    lhsT_scale=scales[u][:, a_cols],
-                    rhs=h_codes[:, h_cols].bitcast(FP8X4),
-                    rhs_scale=h_scales[:, h_cols],
-                    start=(g == 0),
-                    stop=(g == 1),
-                )
-            if i < FILL_ROWS:
-                spare = bank_of(u + 1)[:].rearrange("p q f -> p (q f)")
-                a_cols = slice(2 * q * P, (2 * q + 1) * P)
-                for width in FILL:
+        def multiply_group(u):
+            b = first_row[u] // NB
+            product[u] = product_psum.tile([P, GROUP_SIZES[u], F], F32, name="product")
+            for q in range(GROUP_SIZES[u]):
+                for g in range(PASSES):
+                    a_cols = slice((q * PASSES + g) * P, (q * PASSES + g + 1) * P)
+                    h_cols = slice((b * PASSES + g) * F, (b * PASSES + g + 1) * F)
                     nc.tensor.matmul_mx(
-                        out=spare[:, 0:width],
+                        out=product[u][:, q, :],
                         lhsT=codes[u][:, a_cols].bitcast(FP8X4),
                         lhsT_scale=scales[u][:, a_cols],
-                        rhs=h_codes[:, 0:width].bitcast(FP8X4),
-                        rhs_scale=h_scales[:, 0:width],
-                        start=True,
-                        stop=True,
+                        rhs=h_codes[:, h_cols].bitcast(FP8X4),
+                        rhs_scale=h_scales[:, h_cols],
+                        start=(g == 0),
+                        stop=(g == PASSES - 1),
                     )
 
-        def e_grp(u):
-            i0 = first_row[u]
+        def output_group(u):
+            b, nb = divmod(first_row[u], NB)
             size = GROUP_SIZES[u]
-            b = i0 // NB
-            q0 = i0 % 4
-            o_sb[u] = outp.tile([P, size, F], F32, name="o_sb")
+            result = group_pool.tile([P, size, F], F32, name="result")
             nc.vector.scalar_tensor_tensor(
-                out=o_sb[u][:],
-                in0=o_ps[u][:, 0:size, :],
+                out=result[:],
+                in0=product[u][:],
                 scalar=0.0,
-                in1=bias_f[:].unsqueeze(1).to_broadcast([P, size, F]),
+                in1=bias_f32[:].unsqueeze(1).to_broadcast([P, size, F]),
                 op0=ALU.max,
                 op1=ALU.add,
             )
-            nc.sync.dma_start(out=out_v[b, (i0 // 4) % 2][:, q0 : q0 + size, :], in_=o_sb[u][:])
+            nc.sync.dma_start(out=out_view[b][:, nb : nb + size, :], in_=result[:])
 
-        def hs1(b):
-            xt_ps = pst.tile([P, NB, P], BF16, tag="tp", name="xt_ps")
+        def transpose_x(b):
+            bank = turn_psum.tile([P, NB, P], BF16, tag="turn", name="x_bank")
             for j in range(NB):
-                nc.tensor.transpose(xt_ps[:, j, :], x_sb[:, b * NB + j, :], ident[:])
-            x_t[b] = xtp.tile([P, NB, P], BF16, name="x_t")
-            nc.scalar.copy(out=x_t[b][:], in_=xt_ps[:])
+                nc.tensor.transpose(bank[:, j, :], x_sb[:, b, j, :], identity[:])
+            x_turned[b] = h_pool.tile([P, NB, P], BF16, name="x_turned")
+            nc.scalar.copy(out=x_turned[b][:], in_=bank[:])
 
-        def hs2(b):
-            h_grouped[b] = xtp.tile([P, 2, F, 4], BF16, align_bytes=64, name="h_grouped")
-            for g in range(2):
-                h_ps = pst.tile([P, 4, F], F32, tag="tp", name="h_ps")
+        def multiply_x(b):
+            h_grouped[b] = h_pool.tile([P, PASSES, F, 4], BF16, align_bytes=64, name="h_grouped")
+            for g in range(PASSES):
+                bank = turn_psum.tile([P, 4, F], F32, tag="turn", name="h_bank")
                 for t in range(4):
                     nc.tensor.matmul(
-                        h_ps[:, t, :], lhsT=x_t[b][:, 4 * g + t, :], rhs=w_sb[:], start=True, stop=True
+                        bank[:, t, :], lhsT=x_turned[b][:, 4 * g + t, :], rhs=w_sb[:], start=True, stop=True
                     )
-                nc.scalar.copy(
-                    out=h_grouped[b][:, g, :, :], in_=h_ps[:].rearrange("p t w -> p w t")
-                )
+                nc.scalar.copy(out=h_grouped[b][:, g, :, :], in_=bank[:].rearrange("p t f -> p f t"))
 
-        def hq(b):
-            cols = slice(2 * b * F, 2 * (b + 1) * F)
+        def quantise_h(b):
+            cols = slice(b * PASSES * F, (b + 1) * PASSES * F)
             nc.vector.quantize_mx(
                 out=h_codes[:, cols].bitcast(FP8X4),
                 scales=h_scales[:, cols],
-                in_=h_grouped[b][:].rearrange("p g w t -> p (g w t)"),
+                in_=h_grouped[b][:].rearrange("p g f t -> p (g f t)"),
             )
-
-        plan = {}
-
-        def put(step, kind, args):
-            plan[(step, kind)] = plan.get((step, kind), []) + [args]
-
-        for unit in ((0, 1), (1, 2), (2, 4), (4, 8)):
-            cols = [col_of(0, nb) for nb in range(unit[0], unit[1])]
-            for nb in range(unit[0], unit[1]):
-                if nb in s_rows_of(0):
-                    put(2, "as", (0, nb))
-                else:
-                    put(unit[0], "a", (0, nb))
-            put(unit[0], "loops", (0, unit[0], unit[1]))
-            put(unit[0], "r", (0, min(cols), max(cols) + 1))
-        for b in range(1, B):
-            s_rows = s_rows_of(b)
-            v_rows = [r for r in range(NB) if r not in s_rows]
-            base = NB * (b - 1)
-            if b == 1:
-                s_slots = (5, 6, 6)
-                v_slots = (4, 5, 5, 6, 7)
-            else:
-                s_slots = (2, 4)
-                v_slots = (0, 1, 2, 3, 4, 5, 6, 7)
-            for idx in range(len(s_rows)):
-                put(base + s_slots[idx], "as", (b, s_rows[idx]))
-            for idx in range(len(v_rows)):
-                put(base + v_slots[idx], "a", (b, v_rows[idx]))
-            put(base + 6, "loops", (b, 0, NB))
-            put(base + 7, "r", (b, len(s_rows), len(s_rows) + NB))
-        for b in range(B):
-            put(2 * b + 2, "hs1", b)
-            put(2 * b + 3, "hs2", b)
-            put(2 * b + 6, "hq", b)
 
         load_adj(0, 0, 1)
         load_adj(0, 1, 2)
@@ -326,48 +250,63 @@ def tile_spconvlayer_kernel(tc, x, adj, weight, bias, out):
         load_x(2)
         load_adj(1, 4, 6)
         load_adj(1, 6, 8)
-        load_x(3)
-        for b in range(4, B):
+        for b in range(3, B):
             load_x(b)
-        load_adj(2, 0, 4)
-        load_adj(2, 4, 8)
-        load_adj(3, 0, 4)
-        load_adj(3, 4, 8)
+        for b in range(2, 4):
+            load_adj(b, 0, 4)
+            load_adj(b, 4, 8)
 
-        for s in range(0, ROWS + L_E + 1):
-            for args in plan.get((s, "a"), []):
-                a_row(args[0], args[1])
-            for args in plan.get((s, "loops"), []):
-                self_loops(args[0], args[1], args[2])
-            for args in plan.get((s, "r"), []):
-                r_calc(args[0], args[1], args[2])
-            if s == 2:
-                nc.vector.tensor_copy(out=bias_f[:], in_=bias_bf[:])
-            if s < ROWS:
-                b_row(s)
-                if s % NB == NB - 1 and s // NB + 4 < B:
-                    load_adj(s // NB + 4, 0, 4)
-                    load_adj(s // NB + 4, 4, 8)
-            i = s - L_T
-            if 0 <= i < ROWS:
-                t_row(i)
-            i = s - L_C
-            if 0 <= i < ROWS:
-                c_row(i)
-            for args in plan.get((s, "as"), []):
-                a_row(args[0], args[1])
-            for b in plan.get((s, "hs1"), []):
-                hs1(b)
-            for b in plan.get((s, "hs2"), []):
-                hs2(b)
-            for b in plan.get((s, "hq"), []):
-                hq(b)
-            i = s - L_D
-            if 0 <= i < ROWS and group_of.get(i + 1, -1) != group_of[i]:
-                d_grp(group_of[i])
-            i = s - L_M
-            if 0 <= i < ROWS:
-                mx_row(i)
-            i = s - L_E
-            if 0 <= i < ROWS and group_of.get(i + 1, -1) != group_of[i]:
-                e_grp(group_of[i])
+        half = NB // 2
+        for nb in range(half):
+            sum_rows(0, nb)
+        add_self_loops(0, 0, half)
+        invert_sums(0, 0, half)
+        scale_diagonal(0, 0, half)
+        transpose_x(0)
+
+        for step in range(ROWS + LAG_OUTPUT + 1):
+            b, k = divmod(step, NB)
+            following = b + 1
+            if following < B and k == 7:
+                invert_sums(following, 0, NB)
+            if step < ROWS:
+                scale_rows(step)
+            if step < 2:
+                sum_rows(0, half + step)
+            if step == 2:
+                add_self_loops(0, half, NB)
+                invert_sums(0, half, NB)
+                scale_diagonal(0, half, NB)
+                nc.vector.tensor_copy(out=bias_f32[:], in_=bias_bf16[:])
+            if following < B:
+                if k < VECTOR_SUMS:
+                    sum_rows(following, k)
+                if k == 6:
+                    add_self_loops(following, 0, NB)
+                if k == 7:
+                    scale_diagonal(following, 0, NB)
+            if k == 7 and b + 4 < B:
+                load_adj(b + 4, 0, half)
+                load_adj(b + 4, half, NB)
+            if 0 <= step - LAG_TRANSPOSE < ROWS:
+                transpose_rows(step - LAG_TRANSPOSE)
+            if 0 <= step - LAG_COPY < ROWS:
+                copy_rows(step - LAG_COPY)
+            j, odd = divmod(step, 2)
+            if not odd and j < B:
+                multiply_x(j)
+            if odd and j + 1 < B:
+                transpose_x(j + 1)
+            if odd and 0 <= j - 1 < B:
+                quantise_h(j - 1)
+            if step == 0:
+                sum_rows(0, VECTOR_SUMS)
+                sum_rows(0, VECTOR_SUMS + 1)
+            if following < B and k in (2, 4):
+                sum_rows(following, VECTOR_SUMS + k // 2 - 1)
+            if ends_group(step - LAG_QUANTISE):
+                quantise_group(group_of[step - LAG_QUANTISE])
+            if ends_group(step - LAG_MATMUL):
+                multiply_group(group_of[step - LAG_MATMUL])
+            if ends_group(step - LAG_OUTPUT):
+                output_group(group_of[step - LAG_OUTPUT])

@@ -17,10 +17,11 @@ F = 128
 P = 128
 NB = N // P
 ROWS = B * NB
-PASSES = N // (4 * P)
+PACK = 4
+PASSES = N // (PACK * P)
 FLOPS = 2 * B * N * N * F + 2 * B * N * F * F
 
-VECTOR_SUMS = 6
+VECTOR_SUMS = 5
 GROUP_SIZES = [4] * (ROWS // 4 - 1) + [2, 1, 1]
 LAG_TRANSPOSE = 1
 LAG_COPY = 2
@@ -42,21 +43,21 @@ def tile_spconvlayer_kernel(tc, x, adj, weight, bias, out):
         product_psum = ctx.enter_context(tc.psum_pool(name="product_psum", bufs=2))
         ctx.enter_context(tc.manual_schedule())
 
-        x_view = x.rearrange("b (j p) m a -> b p j (m a)", p=P)
+        x_view = x.rearrange("b (nb p) m a -> b p nb (m a)", p=P)
         adj_view = adj.rearrange("b (nb p) c -> b p nb c", p=P)
-        out_view = out.rearrange("b (nb p) u w -> b p nb (u w)", p=P)
+        out_view = out.rearrange("b (nb p) v w -> b p nb (v w)", p=P)
 
         identity = const.tile([P, P], BF16)
         make_identity(nc, identity[:])
         w_sb = const.tile([P, F], BF16)
         for m in range(4):
             nc.scalar.dma_start(
-                out=w_sb[32 * m : 32 * m + 32, :].rearrange("a (u w) -> a u w", u=4),
-                in_=weight[m].rearrange("u a w -> a u w"),
+                out=w_sb[32 * m : 32 * m + 32, :].rearrange("a (v w) -> a v w", v=4),
+                in_=weight[m].rearrange("v a w -> a v w"),
             )
         bias_bf16 = const.tile([P, F], BF16)
         nc.scalar.dma_start(
-            out=bias_bf16[:], in_=bias.rearrange("o i u w -> (o i u w)").partition_broadcast(P)
+            out=bias_bf16[:], in_=bias.rearrange("o i v w -> (o i v w)").partition_broadcast(P)
         )
         bias_f32 = const.tile([P, F], F32)
         x_sb = const.tile([P, B, NB, F], BF16)
@@ -91,8 +92,8 @@ def tile_spconvlayer_kernel(tc, x, adj, weight, bias, out):
         def load_adj(b, lo, hi):
             if b not in adj_sb:
                 adj_sb[b] = adj_pool.tile([P, (NB + 1) * N], BF16, name="adj_sb")
-            rows = adj_sb[b][:, 0 : NB * N].rearrange("p (nb c) -> p nb c", c=N)
-            nc.sync.dma_start(out=rows[:, lo:hi, :], in_=adj_view[b][:, lo:hi, :])
+            blocks = adj_sb[b][:, 0 : NB * N].rearrange("p (nb c) -> p nb c", c=N)
+            nc.sync.dma_start(out=blocks[:, lo:hi, :], in_=adj_view[b][:, lo:hi, :])
 
         def load_x(b):
             nc.sync.dma_start(out=x_sb[:, b, :, :], in_=x_view[b])
@@ -158,12 +159,13 @@ def tile_spconvlayer_kernel(tc, x, adj, weight, bias, out):
 
         def transpose_rows(i):
             b, nb = divmod(i, NB)
-            turned[i] = turn_psum.tile([P, PASSES, 4, P], BF16, tag="turn", name="turned")
-            for block in range(NB):
-                source = scaled[i][:, block * P : (block + 1) * P]
-                if block == nb:
+            turned[i] = turn_psum.tile([P, PASSES, PACK, P], BF16, tag="turn", name="turned")
+            for square in range(NB):
+                g, t = divmod(square, PACK)
+                source = scaled[i][:, square * P : (square + 1) * P]
+                if square == nb:
                     source = diagonal[b][:, nb, :]
-                nc.tensor.transpose(turned[i][:, block // 4, block % 4, :], source, identity[:])
+                nc.tensor.transpose(turned[i][:, g, t, :], source, identity[:])
 
         def copy_rows(i):
             u = group_of[i]
@@ -171,7 +173,7 @@ def tile_spconvlayer_kernel(tc, x, adj, weight, bias, out):
             if q == 0:
                 grouped[u] = group_pool.tile([P, GROUP_SIZES[u] * N], BF16, align_bytes=64, name="grouped")
             nc.scalar.copy(
-                out=grouped[u][:, q * N : (q + 1) * N].rearrange("p (g n t) -> p g n t", g=PASSES, t=4),
+                out=grouped[u][:, q * N : (q + 1) * N].rearrange("p (g n t) -> p g n t", g=PASSES, t=PACK),
                 in_=turned[i][:].rearrange("p g t n -> p g n t"),
             )
 
@@ -214,18 +216,18 @@ def tile_spconvlayer_kernel(tc, x, adj, weight, bias, out):
 
         def transpose_x(b):
             bank = turn_psum.tile([P, NB, P], BF16, tag="turn", name="x_bank")
-            for j in range(NB):
-                nc.tensor.transpose(bank[:, j, :], x_sb[:, b, j, :], identity[:])
+            for nb in range(NB):
+                nc.tensor.transpose(bank[:, nb, :], x_sb[:, b, nb, :], identity[:])
             x_turned[b] = h_pool.tile([P, NB, P], BF16, name="x_turned")
             nc.scalar.copy(out=x_turned[b][:], in_=bank[:])
 
         def multiply_x(b):
-            h_grouped[b] = h_pool.tile([P, PASSES, F, 4], BF16, align_bytes=64, name="h_grouped")
+            h_grouped[b] = h_pool.tile([P, PASSES, F, PACK], BF16, align_bytes=64, name="h_grouped")
             for g in range(PASSES):
-                bank = turn_psum.tile([P, 4, F], F32, tag="turn", name="h_bank")
-                for t in range(4):
+                bank = turn_psum.tile([P, PACK, F], F32, tag="turn", name="h_bank")
+                for t in range(PACK):
                     nc.tensor.matmul(
-                        bank[:, t, :], lhsT=x_turned[b][:, 4 * g + t, :], rhs=w_sb[:], start=True, stop=True
+                        bank[:, t, :], lhsT=x_turned[b][:, PACK * g + t, :], rhs=w_sb[:], start=True, stop=True
                     )
                 nc.scalar.copy(out=h_grouped[b][:, g, :, :], in_=bank[:].rearrange("p t f -> p f t"))
 
@@ -271,7 +273,7 @@ def tile_spconvlayer_kernel(tc, x, adj, weight, bias, out):
                 invert_sums(following, 0, NB)
             if step < ROWS:
                 scale_rows(step)
-            if step < 2:
+            if step < VECTOR_SUMS - half:
                 sum_rows(0, half + step)
             if step == 2:
                 add_self_loops(0, half, NB)
@@ -292,18 +294,18 @@ def tile_spconvlayer_kernel(tc, x, adj, weight, bias, out):
                 transpose_rows(step - LAG_TRANSPOSE)
             if 0 <= step - LAG_COPY < ROWS:
                 copy_rows(step - LAG_COPY)
-            j, odd = divmod(step, 2)
-            if not odd and j < B:
-                multiply_x(j)
-            if odd and j + 1 < B:
-                transpose_x(j + 1)
-            if odd and 0 <= j - 1 < B:
-                quantise_h(j - 1)
+            item, odd = divmod(step, 2)
+            if not odd and item < B:
+                multiply_x(item)
+            if odd and item + 1 < B:
+                transpose_x(item + 1)
+            if odd and 0 <= item - 1 < B:
+                quantise_h(item - 1)
             if step == 0:
-                sum_rows(0, VECTOR_SUMS)
-                sum_rows(0, VECTOR_SUMS + 1)
-            if following < B and k in (2, 4):
-                sum_rows(following, VECTOR_SUMS + k // 2 - 1)
+                for nb in range(VECTOR_SUMS, NB):
+                    sum_rows(0, nb)
+            if following < B and 2 <= k < 2 + NB - VECTOR_SUMS:
+                sum_rows(following, VECTOR_SUMS + k - 2)
             if ends_group(step - LAG_QUANTISE):
                 quantise_group(group_of[step - LAG_QUANTISE])
             if ends_group(step - LAG_MATMUL):

from contextlib import ExitStack

import concourse.mybir as mybir
from concourse.masks import make_identity

BF16 = mybir.dt.bfloat16
F32 = mybir.dt.float32
U32 = mybir.dt.uint32
U8 = mybir.dt.uint8
FP8X4 = mybir.dt.float8_e4m3fn_x4
ALU = mybir.AluOpType
ACT = mybir.ActivationFunctionType

B = 8
N = 1024
F = 128
P = 128
NB = N // P
ROWS = B * NB
PACK = 4
PASSES = N // (PACK * P)
FLOPS = 2 * B * N * N * F + 2 * B * N * F * F

VECTOR_SUMS = 5
GROUP_SIZES = [4] * (ROWS // 4 - 1) + [2, 1, 1]
LAG_TRANSPOSE = 1
LAG_COPY = 2
LAG_QUANTISE = 4
LAG_MATMUL = 6
LAG_OUTPUT = 8


def tile_spconvlayer_kernel(tc, x, adj, weight, bias, out):
    nc = tc.nc
    with ExitStack() as ctx:
        const = ctx.enter_context(tc.tile_pool(name="const", bufs=1))
        adj_pool = ctx.enter_context(tc.tile_pool(name="adj_pool", bufs=4))
        norm_pool = ctx.enter_context(tc.tile_pool(name="norm_pool", bufs=3))
        scaled_pool = ctx.enter_context(tc.tile_pool(name="scaled_pool", bufs=6))
        group_pool = ctx.enter_context(tc.tile_pool(name="group_pool", bufs=3))
        h_pool = ctx.enter_context(tc.tile_pool(name="h_pool", bufs=3))
        turn_psum = ctx.enter_context(tc.psum_pool(name="turn_psum", bufs=6))
        product_psum = ctx.enter_context(tc.psum_pool(name="product_psum", bufs=2))
        ctx.enter_context(tc.manual_schedule())

        x_view = x.rearrange("b (nb p) m a -> b p nb (m a)", p=P)
        adj_view = adj.rearrange("b (nb p) c -> b p nb c", p=P)
        out_view = out.rearrange("b (nb p) v w -> b p nb (v w)", p=P)

        identity = const.tile([P, P], BF16)
        make_identity(nc, identity[:])
        w_sb = const.tile([P, F], BF16)
        for m in range(4):
            nc.scalar.dma_start(
                out=w_sb[32 * m : 32 * m + 32, :].rearrange("a (v w) -> a v w", v=4),
                in_=weight[m].rearrange("v a w -> a v w"),
            )
        bias_bf16 = const.tile([P, F], BF16)
        nc.scalar.dma_start(
            out=bias_bf16[:], in_=bias.rearrange("o i v w -> (o i v w)").partition_broadcast(P)
        )
        bias_f32 = const.tile([P, F], F32)
        x_sb = const.tile([P, B, NB, F], BF16)
        h_codes = const.tile([P, B * PASSES * F], U32, align_bytes=64)
        h_scales = const.tile([P, B * PASSES * F], U8, align_bytes=64)
        unused_vector = const.tile([P, N], BF16)
        unused_scalar = const.tile([P, N], BF16)

        adj_sb = {}
        sums = {}
        r = {}
        with_loops = {}
        diagonal = {}
        x_turned = {}
        h_grouped = {}
        scaled = {}
        turned = {}
        grouped = {}
        codes = {}
        scales = {}
        product = {}

        first_row = [sum(GROUP_SIZES[:u]) for u in range(len(GROUP_SIZES))]
        group_of = {}
        for u in range(len(GROUP_SIZES)):
            for q in range(GROUP_SIZES[u]):
                group_of[first_row[u] + q] = u

        def ends_group(i):
            return 0 <= i < ROWS and group_of.get(i + 1, -1) != group_of[i]

        def load_adj(b, lo, hi):
            if b not in adj_sb:
                adj_sb[b] = adj_pool.tile([P, (NB + 1) * N], BF16, name="adj_sb")
            blocks = adj_sb[b][:, 0 : NB * N].rearrange("p (nb c) -> p nb c", c=N)
            nc.sync.dma_start(out=blocks[:, lo:hi, :], in_=adj_view[b][:, lo:hi, :])

        def load_x(b):
            nc.sync.dma_start(out=x_sb[:, b, :, :], in_=x_view[b])

        def column(nb):
            return nb + 8 - VECTOR_SUMS

        def sum_rows(b, nb):
            if b not in sums:
                sums[b] = norm_pool.tile([P, 16], F32, name="sums")
            rows = adj_sb[b][:, nb * N : (nb + 1) * N]
            total = sums[b][:, column(nb) : column(nb) + 1]
            if nb < VECTOR_SUMS:
                nc.vector.tensor_scalar(
                    out=unused_vector[:],
                    in0=rows,
                    scalar1=1.0,
                    scalar2=1.0,
                    op0=ALU.mult,
                    op1=ALU.add,
                    accum_out=total,
                )
            else:
                nc.scalar.activation(
                    out=unused_scalar[:], in_=rows, func=ACT.Copy, bias=1.0 / N, accum_out=total
                )

        def add_self_loops(b, lo, hi):
            if b not in with_loops:
                with_loops[b] = norm_pool.tile([P, NB, P], F32, name="with_loops")
            nc.vector.tensor_tensor(
                out=with_loops[b][:, lo:hi, :],
                in0=adj_sb[b][:].rearrange("p (nb c) -> p nb c", c=N + P)[:, lo:hi, 0:P],
                in1=identity[:].unsqueeze(1).to_broadcast([P, hi - lo, P]),
                op=ALU.add,
            )

        def invert_sums(b, lo, hi):
            if b not in r:
                r[b] = norm_pool.tile([P, 16], F32, name="r")
            nc.vector.reciprocal(r[b][:, column(lo) : column(hi)], sums[b][:, column(lo) : column(hi)])

        def scale_diagonal(b, lo, hi):
            if b not in diagonal:
                diagonal[b] = norm_pool.tile([P, NB, P], BF16, name="diagonal")
            nc.vector.tensor_tensor(
                out=diagonal[b][:, lo:hi, :],
                in0=with_loops[b][:, lo:hi, :],
                in1=r[b][:, column(lo) : column(hi)].unsqueeze(2).to_broadcast([P, hi - lo, P]),
                op=ALU.mult,
            )

        def scale_rows(i):
            b, nb = divmod(i, NB)
            scaled[i] = scaled_pool.tile([P, N], BF16, name="scaled")
            nc.vector.tensor_scalar(
                out=scaled[i][:],
                in0=adj_sb[b][:, nb * N : (nb + 1) * N],
                scalar1=r[b][:, column(nb) : column(nb) + 1],
                scalar2=None,
                op0=ALU.mult,
            )

        def transpose_rows(i):
            b, nb = divmod(i, NB)
            turned[i] = turn_psum.tile([P, PASSES, PACK, P], BF16, tag="turn", name="turned")
            for square in range(NB):
                g, t = divmod(square, PACK)
                source = scaled[i][:, square * P : (square + 1) * P]
                if square == nb:
                    source = diagonal[b][:, nb, :]
                nc.tensor.transpose(turned[i][:, g, t, :], source, identity[:])

        def copy_rows(i):
            u = group_of[i]
            q = i - first_row[u]
            if q == 0:
                grouped[u] = group_pool.tile([P, GROUP_SIZES[u] * N], BF16, align_bytes=64, name="grouped")
            nc.scalar.copy(
                out=grouped[u][:, q * N : (q + 1) * N].rearrange("p (g n t) -> p g n t", g=PASSES, t=PACK),
                in_=turned[i][:].rearrange("p g t n -> p g n t"),
            )

        def quantise_group(u):
            width = GROUP_SIZES[u] * PASSES * P
            codes[u] = group_pool.tile([P, width], U32, align_bytes=64, name="codes")
            scales[u] = group_pool.tile([P, width], U8, align_bytes=64, name="scales")
            nc.vector.quantize_mx(out=codes[u][:].bitcast(FP8X4), scales=scales[u][:], in_=grouped[u][:])

        def multiply_group(u):
            b = first_row[u] // NB
            product[u] = product_psum.tile([P, GROUP_SIZES[u], F], F32, name="product")
            for q in range(GROUP_SIZES[u]):
                for g in range(PASSES):
                    a_cols = slice((q * PASSES + g) * P, (q * PASSES + g + 1) * P)
                    h_cols = slice((b * PASSES + g) * F, (b * PASSES + g + 1) * F)
                    nc.tensor.matmul_mx(
                        out=product[u][:, q, :],
                        lhsT=codes[u][:, a_cols].bitcast(FP8X4),
                        lhsT_scale=scales[u][:, a_cols],
                        rhs=h_codes[:, h_cols].bitcast(FP8X4),
                        rhs_scale=h_scales[:, h_cols],
                        start=(g == 0),
                        stop=(g == PASSES - 1),
                    )

        def output_group(u):
            b, nb = divmod(first_row[u], NB)
            size = GROUP_SIZES[u]
            result = group_pool.tile([P, size, F], F32, name="result")
            nc.vector.scalar_tensor_tensor(
                out=result[:],
                in0=product[u][:],
                scalar=0.0,
                in1=bias_f32[:].unsqueeze(1).to_broadcast([P, size, F]),
                op0=ALU.max,
                op1=ALU.add,
            )
            nc.sync.dma_start(out=out_view[b][:, nb : nb + size, :], in_=result[:])

        def transpose_x(b):
            bank = turn_psum.tile([P, NB, P], BF16, tag="turn", name="x_bank")
            for nb in range(NB):
                nc.tensor.transpose(bank[:, nb, :], x_sb[:, b, nb, :], identity[:])
            x_turned[b] = h_pool.tile([P, NB, P], BF16, name="x_turned")
            nc.scalar.copy(out=x_turned[b][:], in_=bank[:])

        def multiply_x(b):
            h_grouped[b] = h_pool.tile([P, PASSES, F, PACK], BF16, align_bytes=64, name="h_grouped")
            for g in range(PASSES):
                bank = turn_psum.tile([P, PACK, F], F32, tag="turn", name="h_bank")
                for t in range(PACK):
                    nc.tensor.matmul(
                        bank[:, t, :], lhsT=x_turned[b][:, PACK * g + t, :], rhs=w_sb[:], start=True, stop=True
                    )
                nc.scalar.copy(out=h_grouped[b][:, g, :, :], in_=bank[:].rearrange("p t f -> p f t"))

        def quantise_h(b):
            cols = slice(b * PASSES * F, (b + 1) * PASSES * F)
            nc.vector.quantize_mx(
                out=h_codes[:, cols].bitcast(FP8X4),
                scales=h_scales[:, cols],
                in_=h_grouped[b][:].rearrange("p g f t -> p (g f t)"),
            )

        load_adj(0, 0, 1)
        load_adj(0, 1, 2)
        load_x(0)
        load_adj(0, 2, 3)
        load_adj(0, 3, 4)
        load_x(1)
        load_adj(0, 4, 6)
        load_adj(0, 6, 8)
        load_adj(1, 0, 2)
        load_adj(1, 2, 4)
        load_x(2)
        load_adj(1, 4, 6)
        load_adj(1, 6, 8)
        for b in range(3, B):
            load_x(b)
        for b in range(2, 4):
            load_adj(b, 0, 4)
            load_adj(b, 4, 8)

        half = NB // 2
        for nb in range(half):
            sum_rows(0, nb)
        add_self_loops(0, 0, half)
        invert_sums(0, 0, half)
        scale_diagonal(0, 0, half)
        transpose_x(0)

        for step in range(ROWS + LAG_OUTPUT + 1):
            b, k = divmod(step, NB)
            following = b + 1
            if following < B and k == 7:
                invert_sums(following, 0, NB)
            if step < ROWS:
                scale_rows(step)
            if step < VECTOR_SUMS - half:
                sum_rows(0, half + step)
            if step == 2:
                add_self_loops(0, half, NB)
                invert_sums(0, half, NB)
                scale_diagonal(0, half, NB)
                nc.vector.tensor_copy(out=bias_f32[:], in_=bias_bf16[:])
            if following < B:
                if k < VECTOR_SUMS:
                    sum_rows(following, k)
                if k == 6:
                    add_self_loops(following, 0, NB)
                if k == 7:
                    scale_diagonal(following, 0, NB)
            if k == 7 and b + 4 < B:
                load_adj(b + 4, 0, half)
                load_adj(b + 4, half, NB)
            if 0 <= step - LAG_TRANSPOSE < ROWS:
                transpose_rows(step - LAG_TRANSPOSE)
            if 0 <= step - LAG_COPY < ROWS:
                copy_rows(step - LAG_COPY)
            item, odd = divmod(step, 2)
            if not odd and item < B:
                multiply_x(item)
            if odd and item + 1 < B:
                transpose_x(item + 1)
            if odd and 0 <= item - 1 < B:
                quantise_h(item - 1)
            if step == 0:
                for nb in range(VECTOR_SUMS, NB):
                    sum_rows(0, nb)
            if following < B and 2 <= k < 2 + NB - VECTOR_SUMS:
                sum_rows(following, VECTOR_SUMS + k - 2)
            if ends_group(step - LAG_QUANTISE):
                quantise_group(group_of[step - LAG_QUANTISE])
            if ends_group(step - LAG_MATMUL):
                multiply_group(group_of[step - LAG_MATMUL])
            if ends_group(step - LAG_OUTPUT):
                output_group(group_of[step - LAG_OUTPUT])
